import numpy as np
import ml_dtypes


def mxq(x, axis, fmt="e4m3"):
    dtype, down = {"e4m3": (ml_dtypes.float8_e4m3fn, 7), "e5m2": (ml_dtypes.float8_e5m2, 14)}[fmt]
    v = np.moveaxis(np.asarray(x, np.float32).astype(ml_dtypes.bfloat16).astype(np.float64), axis, -1)
    blocks = v.reshape(v.shape[:-1] + (-1, 32))
    amax = np.abs(blocks).max(-1, keepdims=True)
    byte = np.maximum(np.where(amax > 0, np.frexp(amax)[1] - 1 + 127, 0) - down, 1)
    scale = np.exp2(byte - 127.0)
    codes = (blocks / scale).astype(np.float32).astype(dtype).astype(np.float64)
    return np.moveaxis((codes * scale).reshape(v.shape), -1, axis)


WIDE = False


def mx_kscale(k):
    if not WIDE:
        return np.ones(k)
    levels = np.array([10, -10, 5, -5, 0])
    a = np.random.permutation(np.resize(levels, k // 512 * 4)).reshape(k // 512, 4)
    idx = np.arange(k)
    return np.exp2(a[idx // 512, idx % 128 // 32])


BF16 = ml_dtypes.bfloat16


def bf(x):
    return np.asarray(x, np.float32).astype(BF16)


def f64(x):
    return np.asarray(x).astype(np.float64)


B, T, C, NH, NKV, HD, W, NG, HID = 4, 2048, 1024, 1, 1, 128, 512, 512, 2752
EPS = 1e-6


def rope(a, fc, fs):
    ae, ao = a[..., 0::2], a[..., 1::2]
    return np.stack([ae * fc - ao * fs, ae * fs + ao * fc], axis=-1).reshape(a.shape)


def setup_inputs():
    s = mx_kscale(C)
    fr = np.outer(np.arange(T), 1.0 / 10000.0 ** (np.arange(0, HD, 2) / HD))
    rows = np.where(np.random.random((B, T, 1)) < 0.125, 1e-3, 1.0)
    return {"x": bf(np.random.standard_normal((B, T, C)) * rows),
            "freqs_cos": bf(np.cos(fr)),
            "freqs_sin": bf(np.sin(fr)),
            "ln_w": bf((1.0 + 0.1 * np.random.standard_normal(C)) * s),
            "wq": bf(np.random.standard_normal((C, NH * HD)) * 2.0 / np.sqrt(C) / s[:, None]),
            "wk": bf(np.random.standard_normal((C, NKV * HD)) / np.sqrt(C) / s[:, None]),
            "wv": bf(np.random.standard_normal((C, NKV * HD)) / np.sqrt(C) / s[:, None])}


def reference(x, freqs_cos, freqs_sin, ln_w, wq, wk, wv):
    x = f64(x)
    fc, fs = f64(freqs_cos), f64(freqs_sin)
    h = x * (1.0 / np.sqrt(np.mean(np.square(x), axis=-1, keepdims=True) + EPS)) * f64(ln_w)
    hq = mxq(h, 2, "e4m3")
    q = (hq @ mxq(f64(wq), 0, "e4m3")).reshape(B, T, NH, HD).transpose(0, 2, 1, 3)
    k = (hq @ mxq(f64(wk), 0, "e4m3")).reshape(B, T, NKV, HD).transpose(0, 2, 1, 3)
    v = (hq @ mxq(f64(wv), 0, "e4m3")).reshape(B, T, NKV, HD).transpose(0, 2, 1, 3)
    return rope(q, fc, fs), rope(k, fc, fs), v

@@ -1,0 +1,261 @@
+from contextlib import ExitStack
+
+import concourse.mybir as mybir
+from concourse.masks import make_identity
+
+F32 = mybir.dt.float32
+BF16 = mybir.dt.bfloat16
+U32 = mybir.dt.uint32
+U8 = mybir.dt.uint8
+FP8X4 = mybir.dt.float8_e4m3fn_x4
+ACT = mybir.ActivationFunctionType
+ALU = mybir.AluOpType
+
+P = 128
+PACK = 4
+K_PASS = P * PACK
+TOKENS = 4 * 2048
+SEQ = 2048
+C = 1024
+PASSES = C // K_PASS
+HD = 128
+EPS = 1e-6
+GROUP = 4
+N_TILES = TOKENS // P
+N_GROUPS = N_TILES // GROUP
+TABLE_TILES = SEQ // P
+STATS_LEAD = 6
+ROTATED = 4 * HD
+W_COLS = ROTATED + HD
+
+FLOPS = 2 * TOKENS * C * 3 * HD
+
+
+def tile_nexamodel_pa_t_kernel(
+    tc, x, freqs_cos, freqs_sin, ln_w, wq, wk, wv, out_0, out_1, out_2
+):
+    nc = tc.nc
+    x_groups = x.flatten_outer_dims().rearrange("(g p n) k -> g p n k", p=P, n=GROUP)
+    out_groups = [
+        o.flatten_outer_dims().rearrange("(g p n) d -> g p n d", p=P, n=GROUP)
+        for o in (out_0, out_1, out_2)
+    ]
+
+    with ExitStack() as ctx:
+        const = ctx.enter_context(tc.tile_pool(name="const", bufs=1))
+        x_pool = ctx.enter_context(tc.tile_pool(name="x", bufs=4))
+        stat_pool = ctx.enter_context(tc.tile_pool(name="stat", bufs=4))
+        scratch_pool = ctx.enter_context(tc.tile_pool(name="scratch", bufs=2))
+        work = ctx.enter_context(tc.tile_pool(name="work", bufs=3))
+        psum_t = ctx.enter_context(tc.psum_pool(name="psum_t", bufs=3))
+        psum_qk = ctx.enter_context(tc.psum_pool(name="psum_qk", bufs=3))
+        psum_v = ctx.enter_context(tc.psum_pool(name="psum_v", bufs=2))
+
+        x_tiles = {}
+        sumsq_tiles = {}
+        inv_rms_tiles = {}
+
+        def load_group(g):
+            xg = x_pool.tile([P, GROUP, C], BF16, name="xg")
+            nc.sync.dma_start(out=xg[:], in_=x_groups[g])
+            x_tiles[g] = xg
+
+        load_group(0)
+        load_group(1)
+
+        ln_w_rows = const.tile([P, C], BF16, name="ln_w_rows")
+        nc.scalar.dma_start(out=ln_w_rows[:], in_=ln_w.partition_broadcast(P))
+        w_raw = const.tile([P, 3, PASSES, PACK, HD], BF16, name="w_raw")
+        for j, w in enumerate((wq, wk, wv)):
+            nc.scalar.dma_start(
+                out=w_raw[:, j], in_=w.rearrange("(g t p) n -> p g t n", t=PACK, p=P)
+            )
+        cos_sin = const.tile([P, 2, TABLE_TILES, HD // 2], BF16, name="cos_sin")
+        for j, f in enumerate((freqs_cos, freqs_sin)):
+            nc.scalar.dma_start(
+                out=cos_sin[:, j].rearrange("p (m n) i -> p m (n i)", n=GROUP),
+                in_=f.rearrange("(m p n) i -> p m (n i)", p=P, n=GROUP),
+            )
+
+        eps = const.tile([P, 1], F32, name="eps")
+        nc.vector.memset(eps[:], EPS)
+        warm = const.tile([P, 1], F32, name="warm")
+        nc.scalar.activation(out=warm[:], in_=eps[:], func=ACT.Sqrt)
+
+        ident = const.tile([P, P], BF16, name="ident")
+        make_identity(nc, ident[:])
+
+        w_grouped = const.tile([P, PASSES, W_COLS, PACK], BF16, name="w_grouped", align_bytes=64)
+        w_codes = const.tile([P, PASSES, W_COLS], U32, name="w_codes", align_bytes=64)
+        w_scales = const.tile([P, PASSES, W_COLS], U8, name="w_scales", align_bytes=64)
+        for g in range(PASSES):
+            for j, first in ((0, 0), (1, HD), (2, ROTATED)):
+                nc.vector.tensor_copy(
+                    out=w_grouped[:, g, first : first + HD, :],
+                    in_=w_raw[:, j, g].rearrange("p t n -> p n t"),
+                )
+            for j, first in ((0, 2 * HD), (1, 3 * HD)):
+                swapped = w_grouped[:, g, first : first + HD, :].rearrange(
+                    "p (i e) t -> p i e t", e=2
+                )
+                plain = w_raw[:, j, g].rearrange("p t (i e) -> p i e t", e=2)
+                for e in range(2):
+                    nc.vector.tensor_copy(out=swapped[:, :, e, :], in_=plain[:, :, 1 - e, :])
+        for g in range(PASSES):
+            for cols in (slice(0, ROTATED), slice(ROTATED, W_COLS)):
+                nc.vector.quantize_mx(
+                    out=w_codes[:, g, cols].bitcast(FP8X4),
+                    scales=w_scales[:, g, cols],
+                    in_=w_grouped[:, g, cols, :].rearrange("p c t -> p (c t)"),
+                )
+
+        tables = const.tile([P, TABLE_TILES, 2, HD], F32, name="tables")
+        pairs = tables[:].rearrange("p m s (i e) -> p m s i e", e=2)
+        for s, e, sign in ((0, 0, 1.0), (0, 1, 1.0), (1, 0, -1.0), (1, 1, 1.0)):
+            nc.gpsimd.tensor_scalar(
+                out=pairs[:, :, s, :, e],
+                in0=cos_sin[:, s],
+                scalar1=sign,
+                scalar2=0.0,
+                op0=ALU.mult,
+                op1=ALU.add,
+            )
+
+        h_tiles = {}
+        hT_tiles = {}
+        grouped_tiles = {}
+        code_tiles = {}
+        acc_v_tiles = {}
+        result_tiles = {}
+
+        def sum_squares(i):
+            g, n = divmod(i, GROUP)
+            if n == 0:
+                sumsq = stat_pool.tile([P, GROUP], F32, name="sumsq")
+                sumsq_tiles[g] = sumsq
+            squares = scratch_pool.tile([P, C], BF16, name="squares")
+            nc.scalar.activation(
+                out=squares[:],
+                in_=x_tiles[g][:, n, :],
+                func=ACT.Square,
+                accum_out=sumsq_tiles[g][:, n : n + 1],
+            )
+
+        def inverse_rms(g):
+            rms = stat_pool.tile([P, GROUP], F32, name="rms")
+            nc.scalar.activation(
+                out=rms[:], in_=sumsq_tiles[g][:], func=ACT.Sqrt, bias=eps[:], scale=1.0 / C
+            )
+            inv_rms = stat_pool.tile([P, GROUP], F32, name="inv_rms")
+            nc.vector.reciprocal(out=inv_rms[:], in_=rms[:])
+            inv_rms_tiles[g] = inv_rms
+
+        def normalise(i):
+            g, n = divmod(i, GROUP)
+            h = work.tile([P, C], BF16, name="h")
+            nc.vector.scalar_tensor_tensor(
+                out=h[:],
+                in0=x_tiles[g][:, n, :],
+                scalar=inv_rms_tiles[g][:, n : n + 1],
+                in1=ln_w_rows[:],
+                op0=ALU.mult,
+                op1=ALU.mult,
+            )
+            h_tiles[i] = h
+
+        def transpose(i):
+            hT = psum_t.tile([P, PASSES * PACK, P], BF16, name="hT")
+            for c in range(PASSES * PACK):
+                nc.tensor.transpose(hT[:, c, :], h_tiles[i][:, c * P : (c + 1) * P], ident[:])
+            hT_tiles[i] = hT
+
+        def regroup(i):
+            grouped = work.tile([P, PASSES, P, PACK], BF16, name="grouped", align_bytes=64)
+            nc.scalar.copy(
+                out=grouped[:], in_=hT_tiles[i][:].rearrange("p (g t) r -> p g r t", t=PACK)
+            )
+            grouped_tiles[i] = grouped
+
+        def quantise(i):
+            codes = work.tile([P, PASSES * P], U32, name="codes", align_bytes=64)
+            scales = work.tile([P, PASSES * P], U8, name="scales", align_bytes=64)
+            nc.vector.quantize_mx(
+                out=codes[:].bitcast(FP8X4),
+                scales=scales[:],
+                in_=grouped_tiles[i][:].rearrange("p g r t -> p (g r t)"),
+            )
+            code_tiles[i] = (codes, scales)
+
+        def project(i):
+            g, n = divmod(i, GROUP)
+            codes, scales = code_tiles[i]
+            if n == 0:
+                acc_v = psum_v.tile([P, GROUP, HD], F32, name="acc_v")
+                acc_v_tiles[g] = acc_v
+            acc_qk = psum_qk.tile([P, ROTATED], F32, name="acc_qk")
+            for out, cols in (
+                (acc_qk[:], slice(0, ROTATED)),
+                (acc_v_tiles[g][:, n, :], slice(ROTATED, W_COLS)),
+            ):
+                for c in range(PASSES):
+                    tokens = slice(c * P, (c + 1) * P)
+                    nc.tensor.matmul_mx(
+                        out=out,
+                        lhsT=codes[:, tokens].bitcast(FP8X4),
+                        lhsT_scale=scales[:, tokens],
+                        rhs=w_codes[:, c, cols].bitcast(FP8X4),
+                        rhs_scale=w_scales[:, c, cols],
+                        start=(c == 0),
+                        stop=(c == PASSES - 1),
+                    )
+            return acc_qk
+
+        def rope(i, acc_qk):
+            g, n = divmod(i, GROUP)
+            if n == 0:
+                rotated = work.tile([P, 2, GROUP, HD], F32, name="rotated")
+                result_tiles[g] = rotated
+            m = (g * GROUP + n) % TABLE_TILES
+            products = work.tile([P, 2, 2, HD], F32, name="products")
+            nc.vector.tensor_tensor(
+                out=products[:],
+                in0=acc_qk[:].rearrange("p (s c d) -> p s c d", s=2, c=2),
+                in1=tables[:, m].unsqueeze(2).to_broadcast([P, 2, 2, HD]),
+                op=ALU.mult,
+            )
+            nc.vector.tensor_tensor(
+                out=result_tiles[g][:, :, n, :],
+                in0=products[:, 0],
+                in1=products[:, 1],
+                op=ALU.add,
+            )
+
+        def store_group(g):
+            v = work.tile([P, GROUP, HD], F32, name="v")
+            nc.scalar.copy(out=v[:], in_=acc_v_tiles[g][:])
+            nc.sync.dma_start(out=out_groups[0][g], in_=result_tiles[g][:, 0])
+            nc.sync.dma_start(out=out_groups[1][g], in_=result_tiles[g][:, 1])
+            nc.sync.dma_start(out=out_groups[2][g], in_=v[:])
+
+        with tc.manual_schedule():
+            for step in range(-STATS_LEAD, N_TILES + 3):
+                ahead, here, back1, back2, back3 = step + STATS_LEAD, step, step - 1, step - 2, step - 3
+                if ahead < N_TILES and ahead % GROUP == 0 and ahead // GROUP + 2 < N_GROUPS:
+                    load_group(ahead // GROUP + 2)
+                if 0 <= back3 < N_TILES:
+                    acc_qk = project(back3)
+                if 0 <= here < N_TILES:
+                    normalise(here)
+                    transpose(here)
+                if 0 <= back1 < N_TILES:
+                    regroup(back1)
+                if 0 <= back2 < N_TILES:
+                    quantise(back2)
+                if 0 <= back3 < N_TILES:
+                    rope(back3, acc_qk)
+                    if back3 % GROUP == GROUP - 1:
+                        store_group(back3 // GROUP)
+                if ahead < N_TILES:
+                    sum_squares(ahead)
+                    if ahead % GROUP == GROUP - 1:
+                        inverse_rms(ahead // GROUP)

@@ -25,6 +25,7 @@ N_TILES = TOKENS // P
 N_GROUPS = N_TILES // GROUP
 TABLE_TILES = SEQ // P
 STATS_LEAD = 6
+SCALAR_SHARE = 2
 ROTATED = 4 * HD
 W_COLS = ROTATED + HD
 
@@ -47,8 +48,8 @@ def tile_nexamodel_pa_t_kernel(
         stat_pool = ctx.enter_context(tc.tile_pool(name="stat", bufs=4))
         scratch_pool = ctx.enter_context(tc.tile_pool(name="scratch", bufs=2))
         work = ctx.enter_context(tc.tile_pool(name="work", bufs=3))
-        psum_t = ctx.enter_context(tc.psum_pool(name="psum_t", bufs=3))
-        psum_qk = ctx.enter_context(tc.psum_pool(name="psum_qk", bufs=3))
+        psum_t = ctx.enter_context(tc.psum_pool(name="psum_t", bufs=4))
+        psum_qk = ctx.enter_context(tc.psum_pool(name="psum_qk", bufs=2))
         psum_v = ctx.enter_context(tc.psum_pool(name="psum_v", bufs=2))
 
         x_tiles = {}
@@ -63,8 +64,6 @@ def tile_nexamodel_pa_t_kernel(
         load_group(0)
         load_group(1)
 
-        ln_w_rows = const.tile([P, C], BF16, name="ln_w_rows")
-        nc.scalar.dma_start(out=ln_w_rows[:], in_=ln_w.partition_broadcast(P))
         w_raw = const.tile([P, 3, PASSES, PACK, HD], BF16, name="w_raw")
         for j, w in enumerate((wq, wk, wv)):
             nc.scalar.dma_start(
@@ -82,8 +81,22 @@ def tile_nexamodel_pa_t_kernel(
         warm = const.tile([P, 1], F32, name="warm")
         nc.scalar.activation(out=warm[:], in_=eps[:], func=ACT.Sqrt)
 
-        ident = const.tile([P, P], BF16, name="ident")
+        ident = const.tile([P, P], F32, name="ident")
         make_identity(nc, ident[:])
+
+        ln_w_rows = const.tile([P, P], BF16, name="ln_w_rows")
+        nc.vector.memset(ln_w_rows[:], 0.0)
+        nc.scalar.dma_start(
+            out=ln_w_rows[0 : C // P, :], in_=ln_w.rearrange("(c p) -> c p", p=P)
+        )
+        ln_w_square = const.tile([P, P], F32, name="ln_w_square")
+        nc.vector.tensor_copy(out=ln_w_square[:], in_=ln_w_rows[:])
+        ln_w_turned = psum_t.tile([P, PACK, P], F32, name="yT")
+        nc.tensor.transpose(ln_w_turned[:, 0, :], ln_w_square[:], ident[:])
+        ln_w_cols = const.tile([P, PASSES, PACK], F32, name="ln_w_cols")
+        nc.vector.tensor_copy(
+            out=ln_w_cols[:].rearrange("p g t -> p (g t)"), in_=ln_w_turned[:, 0, 0 : C // P]
+        )
 
         w_grouped = const.tile([P, PASSES, W_COLS, PACK], BF16, name="w_grouped", align_bytes=64)
         w_codes = const.tile([P, PASSES, W_COLS], U32, name="w_codes", align_bytes=64)
@@ -112,20 +125,14 @@ def tile_nexamodel_pa_t_kernel(
         tables = const.tile([P, TABLE_TILES, 2, HD], F32, name="tables")
         pairs = tables[:].rearrange("p m s (i e) -> p m s i e", e=2)
         for s, e, sign in ((0, 0, 1.0), (0, 1, 1.0), (1, 0, -1.0), (1, 1, 1.0)):
-            nc.gpsimd.tensor_scalar(
-                out=pairs[:, :, s, :, e],
-                in0=cos_sin[:, s],
-                scalar1=sign,
-                scalar2=0.0,
-                op0=ALU.mult,
-                op1=ALU.add,
-            )
+            nc.vector.tensor_scalar_mul(pairs[:, :, s, :, e], cos_sin[:, s], sign)
 
-        h_tiles = {}
-        hT_tiles = {}
+        y_tiles = {}
+        yT_tiles = {}
         grouped_tiles = {}
         code_tiles = {}
         acc_v_tiles = {}
+        product_tiles = {}
         result_tiles = {}
 
         def sum_squares(i):
@@ -150,30 +157,45 @@ def tile_nexamodel_pa_t_kernel(
             nc.vector.reciprocal(out=inv_rms[:], in_=rms[:])
             inv_rms_tiles[g] = inv_rms
 
-        def normalise(i):
+        def scale_rows(i):
             g, n = divmod(i, GROUP)
-            h = work.tile([P, C], BF16, name="h")
-            nc.vector.scalar_tensor_tensor(
-                out=h[:],
-                in0=x_tiles[g][:, n, :],
-                scalar=inv_rms_tiles[g][:, n : n + 1],
-                in1=ln_w_rows[:],
-                op0=ALU.mult,
-                op1=ALU.mult,
-            )
-            h_tiles[i] = h
+            y = work.tile([P, C], F32, name="y")
+            if i % SCALAR_SHARE == 0:
+                nc.scalar.activation(
+                    out=y[:],
+                    in_=x_tiles[g][:, n, :],
+                    func=ACT.Copy,
+                    scale=inv_rms_tiles[g][:, n : n + 1],
+                )
+            else:
+                nc.gpsimd.tensor_scalar(
+                    out=y[:],
+                    in0=x_tiles[g][:, n, :],
+                    scalar1=inv_rms_tiles[g][:, n : n + 1],
+                    scalar2=0.0,
+                    op0=ALU.mult,
+                    op1=ALU.add,
+                )
+            y_tiles[i] = y
 
         def transpose(i):
-            hT = psum_t.tile([P, PASSES * PACK, P], BF16, name="hT")
-            for c in range(PASSES * PACK):
-                nc.tensor.transpose(hT[:, c, :], h_tiles[i][:, c * P : (c + 1) * P], ident[:])
-            hT_tiles[i] = hT
+            yT_tiles[i] = []
+            for g in range(PASSES):
+                yT = psum_t.tile([P, PACK, P], F32, name="yT")
+                for t in range(PACK):
+                    first = g * K_PASS + t * P
+                    nc.tensor.transpose(yT[:, t, :], y_tiles[i][:, first : first + P], ident[:])
+                yT_tiles[i].append(yT)
 
-        def regroup(i):
+        def weigh_and_regroup(i):
             grouped = work.tile([P, PASSES, P, PACK], BF16, name="grouped", align_bytes=64)
-            nc.scalar.copy(
-                out=grouped[:], in_=hT_tiles[i][:].rearrange("p (g t) r -> p g r t", t=PACK)
-            )
+            for g in range(PASSES):
+                nc.vector.tensor_tensor(
+                    out=grouped[:, g],
+                    in0=yT_tiles[i][g][:].rearrange("p t r -> p r t"),
+                    in1=ln_w_cols[:, g].unsqueeze(1).to_broadcast([P, P, PACK]),
+                    op=ALU.mult,
+                )
             grouped_tiles[i] = grouped
 
         def quantise(i):
@@ -210,12 +232,8 @@ def tile_nexamodel_pa_t_kernel(
                     )
             return acc_qk
 
-        def rope(i, acc_qk):
-            g, n = divmod(i, GROUP)
-            if n == 0:
-                rotated = work.tile([P, 2, GROUP, HD], F32, name="rotated")
-                result_tiles[g] = rotated
-            m = (g * GROUP + n) % TABLE_TILES
+        def rope_products(i, acc_qk):
+            m = i % TABLE_TILES
             products = work.tile([P, 2, 2, HD], F32, name="products")
             nc.vector.tensor_tensor(
                 out=products[:],
@@ -223,10 +241,17 @@ def tile_nexamodel_pa_t_kernel(
                 in1=tables[:, m].unsqueeze(2).to_broadcast([P, 2, 2, HD]),
                 op=ALU.mult,
             )
-            nc.vector.tensor_tensor(
+            product_tiles[i] = products
+
+        def rope_sum(i):
+            g, n = divmod(i, GROUP)
+            if n == 0:
+                rotated = work.tile([P, 2, GROUP, HD], F32, name="rotated")
+                result_tiles[g] = rotated
+            nc.gpsimd.tensor_tensor(
                 out=result_tiles[g][:, :, n, :],
-                in0=products[:, 0],
-                in1=products[:, 1],
+                in0=product_tiles[i][:, 0],
+                in1=product_tiles[i][:, 1],
                 op=ALU.add,
             )
 
@@ -237,25 +262,31 @@ def tile_nexamodel_pa_t_kernel(
             nc.sync.dma_start(out=out_groups[1][g], in_=result_tiles[g][:, 1])
             nc.sync.dma_start(out=out_groups[2][g], in_=v[:])
 
+        def exists(i):
+            return 0 <= i < N_TILES
+
         with tc.manual_schedule():
-            for step in range(-STATS_LEAD, N_TILES + 3):
-                ahead, here, back1, back2, back3 = step + STATS_LEAD, step, step - 1, step - 2, step - 3
-                if ahead < N_TILES and ahead % GROUP == 0 and ahead // GROUP + 2 < N_GROUPS:
+            for step in range(-STATS_LEAD, N_TILES + 5):
+                ahead = step + STATS_LEAD
+                if exists(ahead) and ahead % GROUP == 0 and ahead // GROUP + 2 < N_GROUPS:
                     load_group(ahead // GROUP + 2)
-                if 0 <= back3 < N_TILES:
-                    acc_qk = project(back3)
-                if 0 <= here < N_TILES:
-                    normalise(here)
-                    transpose(here)
-                if 0 <= back1 < N_TILES:
-                    regroup(back1)
-                if 0 <= back2 < N_TILES:
-                    quantise(back2)
-                if 0 <= back3 < N_TILES:
-                    rope(back3, acc_qk)
-                    if back3 % GROUP == GROUP - 1:
-                        store_group(back3 // GROUP)
-                if ahead < N_TILES:
+                if exists(step - 3):
+                    acc_qk = project(step - 3)
+                if exists(step):
+                    transpose(step)
+                if exists(step - 1):
+                    weigh_and_regroup(step - 1)
+                if exists(step - 2):
+                    quantise(step - 2)
+                if exists(step - 3):
+                    rope_products(step - 3, acc_qk)
+                if exists(step - 4):
+                    rope_sum(step - 4)
+                    if (step - 4) % GROUP == GROUP - 1:
+                        store_group((step - 4) // GROUP)
+                if exists(step + 1):
+                    scale_rows(step + 1)
+                if exists(ahead):
                     sum_squares(ahead)
                     if ahead % GROUP == GROUP - 1:
                         inverse_rms(ahead // GROUP)

@@ -188,29 +188,33 @@ def tile_nexamodel_pa_t_kernel(
                 yT_tiles[i].append(yT)
 
         def weigh_and_regroup(i):
-            grouped = work.tile([P, PASSES, P, PACK], BF16, name="grouped", align_bytes=64)
+            group, n = divmod(i, GROUP)
+            if n == 0:
+                grouped = work.tile(
+                    [P, GROUP, PASSES, P, PACK], BF16, name="grouped", align_bytes=64
+                )
+                grouped_tiles[group] = grouped
             for g in range(PASSES):
                 nc.vector.tensor_tensor(
-                    out=grouped[:, g],
+                    out=grouped_tiles[group][:, n, g],
                     in0=yT_tiles[i][g][:].rearrange("p t r -> p r t"),
                     in1=ln_w_cols[:, g].unsqueeze(1).to_broadcast([P, P, PACK]),
                     op=ALU.mult,
                 )
-            grouped_tiles[i] = grouped
 
-        def quantise(i):
-            codes = work.tile([P, PASSES * P], U32, name="codes", align_bytes=64)
-            scales = work.tile([P, PASSES * P], U8, name="scales", align_bytes=64)
+        def quantise(group):
+            codes = work.tile([P, GROUP * PASSES * P], U32, name="codes", align_bytes=64)
+            scales = work.tile([P, GROUP * PASSES * P], U8, name="scales", align_bytes=64)
             nc.vector.quantize_mx(
                 out=codes[:].bitcast(FP8X4),
                 scales=scales[:],
-                in_=grouped_tiles[i][:].rearrange("p g r t -> p (g r t)"),
+                in_=grouped_tiles[group][:].rearrange("p n g r t -> p (n g r t)"),
             )
-            code_tiles[i] = (codes, scales)
+            code_tiles[group] = (codes, scales)
 
         def project(i):
             g, n = divmod(i, GROUP)
-            codes, scales = code_tiles[i]
+            codes, scales = code_tiles[g]
             if n == 0:
                 acc_v = psum_v.tile([P, GROUP, HD], F32, name="acc_v")
                 acc_v_tiles[g] = acc_v
@@ -220,7 +224,7 @@ def tile_nexamodel_pa_t_kernel(
                 (acc_v_tiles[g][:, n, :], slice(ROTATED, W_COLS)),
             ):
                 for c in range(PASSES):
-                    tokens = slice(c * P, (c + 1) * P)
+                    tokens = slice((n * PASSES + c) * P, (n * PASSES + c + 1) * P)
                     nc.tensor.matmul_mx(
                         out=out,
                         lhsT=codes[:, tokens].bitcast(FP8X4),
@@ -266,24 +270,24 @@ def tile_nexamodel_pa_t_kernel(
             return 0 <= i < N_TILES
 
         with tc.manual_schedule():
-            for step in range(-STATS_LEAD, N_TILES + 5):
+            for step in range(-STATS_LEAD, N_TILES + 8):
                 ahead = step + STATS_LEAD
                 if exists(ahead) and ahead % GROUP == 0 and ahead // GROUP + 2 < N_GROUPS:
                     load_group(ahead // GROUP + 2)
-                if exists(step - 3):
-                    acc_qk = project(step - 3)
+                if exists(step - 6):
+                    acc_qk = project(step - 6)
                 if exists(step):
                     transpose(step)
                 if exists(step - 1):
                     weigh_and_regroup(step - 1)
-                if exists(step - 2):
-                    quantise(step - 2)
-                if exists(step - 3):
-                    rope_products(step - 3, acc_qk)
-                if exists(step - 4):
-                    rope_sum(step - 4)
-                    if (step - 4) % GROUP == GROUP - 1:
-                        store_group((step - 4) // GROUP)
+                if exists(step - 2) and (step - 2) % GROUP == GROUP - 1:
+                    quantise((step - 2) // GROUP)
+                if exists(step - 6):
+                    rope_products(step - 6, acc_qk)
+                if exists(step - 7):
+                    rope_sum(step - 7)
+                    if (step - 7) % GROUP == GROUP - 1:
+                        store_group((step - 7) // GROUP)
                 if exists(step + 1):
                     scale_rows(step + 1)
                 if exists(ahead):

@@ -25,6 +25,7 @@ N_TILES = TOKENS // P
 N_GROUPS = N_TILES // GROUP
 TABLE_TILES = SEQ // P
 STATS_LEAD = 6
+ROOT_C = 32.0
 SCALAR_SHARE = 2
 ROTATED = 4 * HD
 W_COLS = ROTATED + HD
@@ -61,71 +62,88 @@ def tile_nexamodel_pa_t_kernel(
             nc.sync.dma_start(out=xg[:], in_=x_groups[g])
             x_tiles[g] = xg
 
-        load_group(0)
-        load_group(1)
+        def prepare_constants():
+            one = const.tile([P, 1], F32, name="one")
+            nc.vector.memset(one[:], 1.0)
+            warm = const.tile([P, 1], F32, name="warm")
+            nc.scalar.activation(out=warm[:], in_=one[:], func=ACT.Square)
+            nc.vector.memset(minus_half[:], -0.5)
+            ln_w_rows = const.tile([P, P], BF16, name="ln_w_rows")
+            nc.vector.memset(ln_w_rows[:], 0.0)
 
-        w_raw = const.tile([P, 3, PASSES, PACK, HD], BF16, name="w_raw")
-        for j, w in enumerate((wq, wk, wv)):
-            nc.scalar.dma_start(
-                out=w_raw[:, j], in_=w.rearrange("(g t p) n -> p g t n", t=PACK, p=P)
+            first_group = x_pool.tile([P, GROUP, C], BF16, name="xg")
+            x_tiles[0] = first_group
+            nc.sync.dma_start(out=first_group[:, 0, :], in_=x_groups[0][:, 0, :])
+            cos_sin = const.tile([P, 2, TABLE_TILES, HD // 2], BF16, name="cos_sin")
+            for j, f in enumerate((freqs_cos, freqs_sin)):
+                nc.sync.dma_start(
+                    out=cos_sin[:, j].rearrange("p (m n) i -> p m (n i)", n=GROUP),
+                    in_=f.rearrange("(m p n) i -> p m (n i)", p=P, n=GROUP),
+                )
+            nc.sync.dma_start(
+                out=ln_w_rows[0 : C // P, :], in_=ln_w.rearrange("(c p) -> c p", p=P)
             )
-        cos_sin = const.tile([P, 2, TABLE_TILES, HD // 2], BF16, name="cos_sin")
-        for j, f in enumerate((freqs_cos, freqs_sin)):
-            nc.scalar.dma_start(
-                out=cos_sin[:, j].rearrange("p (m n) i -> p m (n i)", n=GROUP),
-                in_=f.rearrange("(m p n) i -> p m (n i)", p=P, n=GROUP),
+            nc.sync.dma_start(out=first_group[:, 1, :], in_=x_groups[0][:, 1, :])
+            w_raw = const.tile([P, 3, PASSES, PACK, HD], BF16, name="w_raw")
+            for j, w in enumerate((wq, wk, wv)):
+                nc.sync.dma_start(
+                    out=w_raw[:, j], in_=w.rearrange("(g t p) n -> p g t n", t=PACK, p=P)
+                )
+            nc.sync.dma_start(out=first_group[:, 2, :], in_=x_groups[0][:, 2, :])
+            nc.sync.dma_start(out=first_group[:, 3, :], in_=x_groups[0][:, 3, :])
+            load_group(1)
+
+            make_identity(nc, ident[:])
+
+            nc.gpsimd.tensor_scalar(
+                out=tables[:].rearrange("p s m (i e) -> p (s m i) e", e=2),
+                in0=cos_sin[:]
+                .rearrange("p s m i -> p (s m i)")
+                .unsqueeze(2)
+                .to_broadcast([P, 2 * TABLE_TILES * HD // 2, 2]),
+                scalar1=1.0,
+                scalar2=0.0,
+                op0=ALU.mult,
+                op1=ALU.add,
             )
 
-        eps = const.tile([P, 1], F32, name="eps")
-        nc.vector.memset(eps[:], EPS)
-        warm = const.tile([P, 1], F32, name="warm")
-        nc.scalar.activation(out=warm[:], in_=eps[:], func=ACT.Sqrt)
+            ln_w_square = const.tile([P, P], F32, name="ln_w_square")
+            nc.vector.tensor_copy(out=ln_w_square[:], in_=ln_w_rows[:])
+            ln_w_turned = psum_t.tile([P, PACK, P], F32, name="yT")
+            nc.tensor.transpose(ln_w_turned[:, 0, :], ln_w_square[:], ident[:])
 
-        ident = const.tile([P, P], F32, name="ident")
-        make_identity(nc, ident[:])
-
-        ln_w_rows = const.tile([P, P], BF16, name="ln_w_rows")
-        nc.vector.memset(ln_w_rows[:], 0.0)
-        nc.scalar.dma_start(
-            out=ln_w_rows[0 : C // P, :], in_=ln_w.rearrange("(c p) -> c p", p=P)
-        )
-        ln_w_square = const.tile([P, P], F32, name="ln_w_square")
-        nc.vector.tensor_copy(out=ln_w_square[:], in_=ln_w_rows[:])
-        ln_w_turned = psum_t.tile([P, PACK, P], F32, name="yT")
-        nc.tensor.transpose(ln_w_turned[:, 0, :], ln_w_square[:], ident[:])
-        ln_w_cols = const.tile([P, PASSES, PACK], F32, name="ln_w_cols")
-        nc.vector.tensor_copy(
-            out=ln_w_cols[:].rearrange("p g t -> p (g t)"), in_=ln_w_turned[:, 0, 0 : C // P]
-        )
-
-        w_grouped = const.tile([P, PASSES, W_COLS, PACK], BF16, name="w_grouped", align_bytes=64)
-        w_codes = const.tile([P, PASSES, W_COLS], U32, name="w_codes", align_bytes=64)
-        w_scales = const.tile([P, PASSES, W_COLS], U8, name="w_scales", align_bytes=64)
-        for g in range(PASSES):
+            w_grouped = const.tile(
+                [P, PASSES, W_COLS, PACK], BF16, name="w_grouped", align_bytes=64
+            )
             for j, first in ((0, 0), (1, HD), (2, ROTATED)):
                 nc.vector.tensor_copy(
-                    out=w_grouped[:, g, first : first + HD, :],
-                    in_=w_raw[:, j, g].rearrange("p t n -> p n t"),
+                    out=w_grouped[:, :, first : first + HD, :],
+                    in_=w_raw[:, j].rearrange("p g t n -> p g n t"),
                 )
             for j, first in ((0, 2 * HD), (1, 3 * HD)):
-                swapped = w_grouped[:, g, first : first + HD, :].rearrange(
-                    "p (i e) t -> p i e t", e=2
+                turned = w_grouped[:, :, first : first + HD, :].rearrange(
+                    "p g (i e) t -> p g i e t", e=2
                 )
-                plain = w_raw[:, j, g].rearrange("p t (i e) -> p i e t", e=2)
-                for e in range(2):
-                    nc.vector.tensor_copy(out=swapped[:, :, e, :], in_=plain[:, :, 1 - e, :])
-        for g in range(PASSES):
-            for cols in (slice(0, ROTATED), slice(ROTATED, W_COLS)):
-                nc.vector.quantize_mx(
-                    out=w_codes[:, g, cols].bitcast(FP8X4),
-                    scales=w_scales[:, g, cols],
-                    in_=w_grouped[:, g, cols, :].rearrange("p c t -> p (c t)"),
-                )
+                plain = w_raw[:, j].rearrange("p g t (i e) -> p g i e t", e=2)
+                nc.vector.tensor_scalar_mul(turned[:, :, :, 0, :], plain[:, :, :, 1, :], -1.0)
+                nc.vector.tensor_copy(out=turned[:, :, :, 1, :], in_=plain[:, :, :, 0, :])
+            nc.vector.tensor_scalar_mul(
+                ln_w_cols[:].rearrange("p g t -> p (g t)"), ln_w_turned[:, 0, 0 : C // P], ROOT_C
+            )
+            for g in range(PASSES):
+                for cols in (slice(0, ROTATED), slice(ROTATED, W_COLS)):
+                    nc.vector.quantize_mx(
+                        out=w_codes[:, g, cols].bitcast(FP8X4),
+                        scales=w_scales[:, g, cols],
+                        in_=w_grouped[:, g, cols, :].rearrange("p c t -> p (c t)"),
+                    )
 
-        tables = const.tile([P, TABLE_TILES, 2, HD], F32, name="tables")
-        pairs = tables[:].rearrange("p m s (i e) -> p m s i e", e=2)
-        for s, e, sign in ((0, 0, 1.0), (0, 1, 1.0), (1, 0, -1.0), (1, 1, 1.0)):
-            nc.vector.tensor_scalar_mul(pairs[:, :, s, :, e], cos_sin[:, s], sign)
+        ident = const.tile([P, P], F32, name="ident")
+        minus_half = const.tile([P, GROUP], F32, name="minus_half")
+        tables = const.tile([P, 2, TABLE_TILES, HD], F32, name="tables")
+        ln_w_cols = const.tile([P, PASSES, PACK], F32, name="ln_w_cols")
+        w_codes = const.tile([P, PASSES, W_COLS], U32, name="w_codes", align_bytes=64)
+        w_scales = const.tile([P, PASSES, W_COLS], U8, name="w_scales", align_bytes=64)
 
         y_tiles = {}
         yT_tiles = {}
@@ -149,12 +167,19 @@ def tile_nexamodel_pa_t_kernel(
             )
 
         def inverse_rms(g):
-            rms = stat_pool.tile([P, GROUP], F32, name="rms")
-            nc.scalar.activation(
-                out=rms[:], in_=sumsq_tiles[g][:], func=ACT.Sqrt, bias=eps[:], scale=1.0 / C
+            shifted = stat_pool.tile([P, GROUP], F32, name="shifted")
+            nc.gpsimd.tensor_scalar(
+                out=shifted[:],
+                in0=sumsq_tiles[g][:],
+                scalar1=1.0,
+                scalar2=C * EPS,
+                op0=ALU.mult,
+                op1=ALU.add,
             )
             inv_rms = stat_pool.tile([P, GROUP], F32, name="inv_rms")
-            nc.vector.reciprocal(out=inv_rms[:], in_=rms[:])
+            nc.gpsimd.tensor_tensor(
+                out=inv_rms[:], in0=shifted[:], in1=minus_half[:], op=ALU.pow
+            )
             inv_rms_tiles[g] = inv_rms
 
         def scale_rows(i):
@@ -242,7 +267,7 @@ def tile_nexamodel_pa_t_kernel(
             nc.vector.tensor_tensor(
                 out=products[:],
                 in0=acc_qk[:].rearrange("p (s c d) -> p s c d", s=2, c=2),
-                in1=tables[:, m].unsqueeze(2).to_broadcast([P, 2, 2, HD]),
+                in1=tables[:, :, m, :].unsqueeze(2).to_broadcast([P, 2, 2, HD]),
                 op=ALU.mult,
             )
             product_tiles[i] = products
@@ -270,6 +295,7 @@ def tile_nexamodel_pa_t_kernel(
             return 0 <= i < N_TILES
 
         with tc.manual_schedule():
+            prepare_constants()
             for step in range(-STATS_LEAD, N_TILES + 8):
                 ahead = step + STATS_LEAD
                 if exists(ahead) and ahead % GROUP == 0 and ahead // GROUP + 2 < N_GROUPS:

@@ -25,8 +25,7 @@ N_TILES = TOKENS // P
 N_GROUPS = N_TILES // GROUP
 TABLE_TILES = SEQ // P
 STATS_LEAD = 6
-ROOT_C = 32.0
-SCALAR_SHARE = 2
+SCALAR_TILE = 2
 ROTATED = 4 * HD
 W_COLS = ROTATED + HD
 
@@ -63,11 +62,9 @@ def tile_nexamodel_pa_t_kernel(
             x_tiles[g] = xg
 
         def prepare_constants():
-            one = const.tile([P, 1], F32, name="one")
-            nc.vector.memset(one[:], 1.0)
+            nc.vector.memset(eps[:], EPS)
             warm = const.tile([P, 1], F32, name="warm")
-            nc.scalar.activation(out=warm[:], in_=one[:], func=ACT.Square)
-            nc.vector.memset(minus_half[:], -0.5)
+            nc.scalar.activation(out=warm[:], in_=eps[:], func=ACT.Sqrt)
             ln_w_rows = const.tile([P, P], BF16, name="ln_w_rows")
             nc.vector.memset(ln_w_rows[:], 0.0)
 
@@ -92,6 +89,7 @@ def tile_nexamodel_pa_t_kernel(
             nc.sync.dma_start(out=first_group[:, 2, :], in_=x_groups[0][:, 2, :])
             nc.sync.dma_start(out=first_group[:, 3, :], in_=x_groups[0][:, 3, :])
             load_group(1)
+            load_group(2)
 
             make_identity(nc, ident[:])
 
@@ -112,9 +110,6 @@ def tile_nexamodel_pa_t_kernel(
             ln_w_turned = psum_t.tile([P, PACK, P], F32, name="yT")
             nc.tensor.transpose(ln_w_turned[:, 0, :], ln_w_square[:], ident[:])
 
-            w_grouped = const.tile(
-                [P, PASSES, W_COLS, PACK], BF16, name="w_grouped", align_bytes=64
-            )
             for j, first in ((0, 0), (1, HD), (2, ROTATED)):
                 nc.vector.tensor_copy(
                     out=w_grouped[:, :, first : first + HD, :],
@@ -127,9 +122,11 @@ def tile_nexamodel_pa_t_kernel(
                 plain = w_raw[:, j].rearrange("p g t (i e) -> p g i e t", e=2)
                 nc.vector.tensor_scalar_mul(turned[:, :, :, 0, :], plain[:, :, :, 1, :], -1.0)
                 nc.vector.tensor_copy(out=turned[:, :, :, 1, :], in_=plain[:, :, :, 0, :])
-            nc.vector.tensor_scalar_mul(
-                ln_w_cols[:].rearrange("p g t -> p (g t)"), ln_w_turned[:, 0, 0 : C // P], ROOT_C
+            nc.vector.tensor_copy(
+                out=ln_w_cols[:].rearrange("p g t -> p (g t)"), in_=ln_w_turned[:, 0, 0 : C // P]
             )
+
+        def quantise_weights():
             for g in range(PASSES):
                 for cols in (slice(0, ROTATED), slice(ROTATED, W_COLS)):
                     nc.vector.quantize_mx(
@@ -139,7 +136,8 @@ def tile_nexamodel_pa_t_kernel(
                     )
 
         ident = const.tile([P, P], F32, name="ident")
-        minus_half = const.tile([P, GROUP], F32, name="minus_half")
+        eps = const.tile([P, 1], F32, name="eps")
+        w_grouped = const.tile([P, PASSES, W_COLS, PACK], BF16, name="w_grouped", align_bytes=64)
         tables = const.tile([P, 2, TABLE_TILES, HD], F32, name="tables")
         ln_w_cols = const.tile([P, PASSES, PACK], F32, name="ln_w_cols")
         w_codes = const.tile([P, PASSES, W_COLS], U32, name="w_codes", align_bytes=64)
@@ -167,25 +165,18 @@ def tile_nexamodel_pa_t_kernel(
             )
 
         def inverse_rms(g):
-            shifted = stat_pool.tile([P, GROUP], F32, name="shifted")
-            nc.gpsimd.tensor_scalar(
-                out=shifted[:],
-                in0=sumsq_tiles[g][:],
-                scalar1=1.0,
-                scalar2=C * EPS,
-                op0=ALU.mult,
-                op1=ALU.add,
+            rms = stat_pool.tile([P, GROUP], F32, name="rms")
+            nc.scalar.activation(
+                out=rms[:], in_=sumsq_tiles[g][:], func=ACT.Sqrt, bias=eps[:], scale=1.0 / C
             )
             inv_rms = stat_pool.tile([P, GROUP], F32, name="inv_rms")
-            nc.gpsimd.tensor_tensor(
-                out=inv_rms[:], in0=shifted[:], in1=minus_half[:], op=ALU.pow
-            )
+            nc.vector.reciprocal(out=inv_rms[:], in_=rms[:])
             inv_rms_tiles[g] = inv_rms
 
         def scale_rows(i):
             g, n = divmod(i, GROUP)
             y = work.tile([P, C], F32, name="y")
-            if i % SCALAR_SHARE == 0:
+            if n == SCALAR_TILE:
                 nc.scalar.activation(
                     out=y[:],
                     in_=x_tiles[g][:, n, :],
@@ -296,7 +287,11 @@ def tile_nexamodel_pa_t_kernel(
 
         with tc.manual_schedule():
             prepare_constants()
-            for step in range(-STATS_LEAD, N_TILES + 8):
+            for i in range(GROUP):
+                sum_squares(i)
+            inverse_rms(0)
+            quantise_weights()
+            for step in range(GROUP - STATS_LEAD, N_TILES + 8):
                 ahead = step + STATS_LEAD
                 if exists(ahead) and ahead % GROUP == 0 and ahead // GROUP + 2 < N_GROUPS:
                     load_group(ahead // GROUP + 2)

@@ -25,7 +25,7 @@ N_TILES = TOKENS // P
 N_GROUPS = N_TILES // GROUP
 TABLE_TILES = SEQ // P
 STATS_LEAD = 6
-SCALAR_TILE = 2
+SCALAR_TILES = (0, 2)
 ROTATED = 4 * HD
 W_COLS = ROTATED + HD
 
@@ -176,7 +176,7 @@ def tile_nexamodel_pa_t_kernel(
         def scale_rows(i):
             g, n = divmod(i, GROUP)
             y = work.tile([P, C], F32, name="y")
-            if n == SCALAR_TILE:
+            if n in SCALAR_TILES:
                 nc.scalar.activation(
                     out=y[:],
                     in_=x_tiles[g][:, n, :],

@@ -14,6 +14,7 @@ ALU = mybir.AluOpType
 P = 128
 PACK = 4
 K_PASS = P * PACK
+PAIR = 2
 TOKENS = 4 * 2048
 SEQ = 2048
 C = 1024
@@ -24,8 +25,9 @@ GROUP = 4
 N_TILES = TOKENS // P
 N_GROUPS = N_TILES // GROUP
 TABLE_TILES = SEQ // P
-STATS_LEAD = 6
-SCALAR_TILES = (0, 2)
+QUANT_TILES = 2
+STATS_LEAD = 3
+PROJECT_LAG = 3
 ROTATED = 4 * HD
 W_COLS = ROTATED + HD
 
@@ -48,9 +50,18 @@ def tile_nexamodel_pa_t_kernel(
         stat_pool = ctx.enter_context(tc.tile_pool(name="stat", bufs=4))
         scratch_pool = ctx.enter_context(tc.tile_pool(name="scratch", bufs=2))
         work = ctx.enter_context(tc.tile_pool(name="work", bufs=3))
-        psum_t = ctx.enter_context(tc.psum_pool(name="psum_t", bufs=4))
-        psum_qk = ctx.enter_context(tc.psum_pool(name="psum_qk", bufs=2))
+        psum_t = ctx.enter_context(tc.psum_pool(name="psum_t", bufs=3))
+        psum_qk = ctx.enter_context(tc.psum_pool(name="psum_qk", bufs=3))
         psum_v = ctx.enter_context(tc.psum_pool(name="psum_v", bufs=2))
+
+        eps = const.tile([P, 1], F32, name="eps")
+        ident = const.tile([P, P], F32, name="ident")
+        ln_w_rows = const.tile([P, C], BF16, name="ln_w_rows")
+        cos_sin = const.tile([P, 2, TABLE_TILES, HD // 2], BF16, name="cos_sin")
+        w_raw = const.tile([P, 3, PASSES, PACK, HD], BF16, name="w_raw")
+        w_grouped = const.tile([P, PASSES, W_COLS, PACK], BF16, name="w_grouped", align_bytes=64)
+        w_codes = const.tile([P, PASSES, W_COLS], U32, name="w_codes", align_bytes=64)
+        w_scales = const.tile([P, PASSES, W_COLS], U8, name="w_scales", align_bytes=64)
 
         x_tiles = {}
         sumsq_tiles = {}
@@ -61,69 +72,57 @@ def tile_nexamodel_pa_t_kernel(
             nc.sync.dma_start(out=xg[:], in_=x_groups[g])
             x_tiles[g] = xg
 
-        def prepare_constants():
-            nc.vector.memset(eps[:], EPS)
-            warm = const.tile([P, 1], F32, name="warm")
-            nc.scalar.activation(out=warm[:], in_=eps[:], func=ACT.Sqrt)
-            ln_w_rows = const.tile([P, P], BF16, name="ln_w_rows")
-            nc.vector.memset(ln_w_rows[:], 0.0)
-
+        def start_loads():
             first_group = x_pool.tile([P, GROUP, C], BF16, name="xg")
             x_tiles[0] = first_group
-            nc.sync.dma_start(out=first_group[:, 0, :], in_=x_groups[0][:, 0, :])
-            cos_sin = const.tile([P, 2, TABLE_TILES, HD // 2], BF16, name="cos_sin")
+
+            def load_tile(n):
+                nc.sync.dma_start(out=first_group[:, n, :], in_=x_groups[0][:, n, :])
+
+            def load_weight(j, w):
+                nc.sync.dma_start(
+                    out=w_raw[:, j], in_=w.rearrange("(g p t) n -> p g t n", t=PACK, p=P)
+                )
+
+            load_tile(0)
+            load_tile(1)
+            load_weight(0, wq)
+            load_weight(1, wk)
+            nc.sync.dma_start(out=ln_w_rows[:], in_=ln_w.partition_broadcast(P))
+            load_tile(2)
+            load_weight(2, wv)
+            load_tile(3)
             for j, f in enumerate((freqs_cos, freqs_sin)):
                 nc.sync.dma_start(
                     out=cos_sin[:, j].rearrange("p (m n) i -> p m (n i)", n=GROUP),
                     in_=f.rearrange("(m p n) i -> p m (n i)", p=P, n=GROUP),
                 )
-            nc.sync.dma_start(
-                out=ln_w_rows[0 : C // P, :], in_=ln_w.rearrange("(c p) -> c p", p=P)
-            )
-            nc.sync.dma_start(out=first_group[:, 1, :], in_=x_groups[0][:, 1, :])
-            w_raw = const.tile([P, 3, PASSES, PACK, HD], BF16, name="w_raw")
-            for j, w in enumerate((wq, wk, wv)):
-                nc.sync.dma_start(
-                    out=w_raw[:, j], in_=w.rearrange("(g t p) n -> p g t n", t=PACK, p=P)
-                )
-            nc.sync.dma_start(out=first_group[:, 2, :], in_=x_groups[0][:, 2, :])
-            nc.sync.dma_start(out=first_group[:, 3, :], in_=x_groups[0][:, 3, :])
             load_group(1)
             load_group(2)
 
-            make_identity(nc, ident[:])
-
-            nc.gpsimd.tensor_scalar(
-                out=tables[:].rearrange("p s m (i e) -> p (s m i) e", e=2),
-                in0=cos_sin[:]
-                .rearrange("p s m i -> p (s m i)")
-                .unsqueeze(2)
-                .to_broadcast([P, 2 * TABLE_TILES * HD // 2, 2]),
-                scalar1=1.0,
-                scalar2=0.0,
-                op0=ALU.mult,
-                op1=ALU.add,
+        def group_weights():
+            rotated = w_grouped[:, :, 0:ROTATED, :].rearrange(
+                "p g (s i c e) t -> p g s i c e t", s=2, c=2, e=2
             )
-
-            ln_w_square = const.tile([P, P], F32, name="ln_w_square")
-            nc.vector.tensor_copy(out=ln_w_square[:], in_=ln_w_rows[:])
-            ln_w_turned = psum_t.tile([P, PACK, P], F32, name="yT")
-            nc.tensor.transpose(ln_w_turned[:, 0, :], ln_w_square[:], ident[:])
-
-            for j, first in ((0, 0), (1, HD), (2, ROTATED)):
-                nc.vector.tensor_copy(
-                    out=w_grouped[:, :, first : first + HD, :],
-                    in_=w_raw[:, j].rearrange("p g t n -> p g n t"),
-                )
-            for j, first in ((0, 2 * HD), (1, 3 * HD)):
-                turned = w_grouped[:, :, first : first + HD, :].rearrange(
-                    "p g (i e) t -> p g i e t", e=2
-                )
+            for j in (0, 1):
+                for g in range(PASSES):
+                    nc.vector.tensor_copy(
+                        out=rotated[:, g, 0, :, j],
+                        in_=w_raw[:, j, g].rearrange("p t (i e) -> p i e t", e=2),
+                    )
                 plain = w_raw[:, j].rearrange("p g t (i e) -> p g i e t", e=2)
-                nc.vector.tensor_scalar_mul(turned[:, :, :, 0, :], plain[:, :, :, 1, :], -1.0)
-                nc.vector.tensor_copy(out=turned[:, :, :, 1, :], in_=plain[:, :, :, 0, :])
+                for e, sign in ((0, -1.0), (1, 1.0)):
+                    nc.gpsimd.tensor_scalar(
+                        out=rotated[:, :, 1, :, j, e, :],
+                        in0=plain[:, :, :, 1 - e, :],
+                        scalar1=sign,
+                        scalar2=0.0,
+                        op0=ALU.mult,
+                        op1=ALU.add,
+                    )
             nc.vector.tensor_copy(
-                out=ln_w_cols[:].rearrange("p g t -> p (g t)"), in_=ln_w_turned[:, 0, 0 : C // P]
+                out=w_grouped[:, :, ROTATED:W_COLS, :],
+                in_=w_raw[:, 2].rearrange("p g t n -> p g n t"),
             )
 
         def quantise_weights():
@@ -135,112 +134,104 @@ def tile_nexamodel_pa_t_kernel(
                         in_=w_grouped[:, g, cols, :].rearrange("p c t -> p (c t)"),
                     )
 
-        ident = const.tile([P, P], F32, name="ident")
-        eps = const.tile([P, 1], F32, name="eps")
-        w_grouped = const.tile([P, PASSES, W_COLS, PACK], BF16, name="w_grouped", align_bytes=64)
-        tables = const.tile([P, 2, TABLE_TILES, HD], F32, name="tables")
-        ln_w_cols = const.tile([P, PASSES, PACK], F32, name="ln_w_cols")
-        w_codes = const.tile([P, PASSES, W_COLS], U32, name="w_codes", align_bytes=64)
-        w_scales = const.tile([P, PASSES, W_COLS], U8, name="w_scales", align_bytes=64)
-
-        y_tiles = {}
-        yT_tiles = {}
+        h_tiles = {}
+        hT_tiles = {}
         grouped_tiles = {}
         code_tiles = {}
+        acc_qk_tiles = {}
         acc_v_tiles = {}
         product_tiles = {}
         result_tiles = {}
 
         def sum_squares(i):
             g, n = divmod(i, GROUP)
-            if n == 0:
-                sumsq = stat_pool.tile([P, GROUP], F32, name="sumsq")
-                sumsq_tiles[g] = sumsq
+            m, r = divmod(i, QUANT_TILES)
+            if r == 0:
+                sumsq = stat_pool.tile([P, QUANT_TILES], F32, name="sumsq")
+                sumsq_tiles[m] = sumsq
             squares = scratch_pool.tile([P, C], BF16, name="squares")
             nc.scalar.activation(
                 out=squares[:],
                 in_=x_tiles[g][:, n, :],
                 func=ACT.Square,
-                accum_out=sumsq_tiles[g][:, n : n + 1],
+                accum_out=sumsq_tiles[m][:, r : r + 1],
             )
 
-        def inverse_rms(g):
-            rms = stat_pool.tile([P, GROUP], F32, name="rms")
+        def inverse_rms(m):
+            inv_rms = stat_pool.tile([P, QUANT_TILES], F32, name="inv_rms")
             nc.scalar.activation(
-                out=rms[:], in_=sumsq_tiles[g][:], func=ACT.Sqrt, bias=eps[:], scale=1.0 / C
+                out=inv_rms[:],
+                in_=sumsq_tiles[m][:],
+                func=ACT.Abs_reciprocal_sqrt,
+                bias=eps[:],
+                scale=1.0 / C,
             )
-            inv_rms = stat_pool.tile([P, GROUP], F32, name="inv_rms")
-            nc.vector.reciprocal(out=inv_rms[:], in_=rms[:])
-            inv_rms_tiles[g] = inv_rms
+            inv_rms_tiles[m] = inv_rms
 
-        def scale_rows(i):
+        def normalise(i):
             g, n = divmod(i, GROUP)
-            y = work.tile([P, C], F32, name="y")
-            if n in SCALAR_TILES:
-                nc.scalar.activation(
-                    out=y[:],
-                    in_=x_tiles[g][:, n, :],
-                    func=ACT.Copy,
-                    scale=inv_rms_tiles[g][:, n : n + 1],
-                )
-            else:
-                nc.gpsimd.tensor_scalar(
-                    out=y[:],
-                    in0=x_tiles[g][:, n, :],
-                    scalar1=inv_rms_tiles[g][:, n : n + 1],
-                    scalar2=0.0,
-                    op0=ALU.mult,
-                    op1=ALU.add,
-                )
-            y_tiles[i] = y
+            m, r = divmod(i, QUANT_TILES)
+            h = work.tile([P, C], BF16, name="h")
+            nc.vector.scalar_tensor_tensor(
+                out=h[:],
+                in0=x_tiles[g][:, n, :],
+                scalar=inv_rms_tiles[m][:, r : r + 1],
+                in1=ln_w_rows[:],
+                op0=ALU.mult,
+                op1=ALU.mult,
+            )
+            h_tiles[i] = h
 
         def transpose(i):
-            yT_tiles[i] = []
+            words = h_tiles[i][:].bitcast(F32)
+            hT = psum_t.tile([P, PASSES * PAIR, P], F32, name="hT")
+            pass_words = K_PASS // PAIR
             for g in range(PASSES):
-                yT = psum_t.tile([P, PACK, P], F32, name="yT")
-                for t in range(PACK):
-                    first = g * K_PASS + t * P
-                    nc.tensor.transpose(yT[:, t, :], y_tiles[i][:, first : first + P], ident[:])
-                yT_tiles[i].append(yT)
+                for u in range(PAIR):
+                    nc.tensor.transpose(
+                        hT[:, g * PAIR + u, :],
+                        words[:, g * pass_words + u : (g + 1) * pass_words : PAIR],
+                        ident[:],
+                    )
+            hT_tiles[i] = hT
 
-        def weigh_and_regroup(i):
-            group, n = divmod(i, GROUP)
-            if n == 0:
+        def regroup(i):
+            m, r = divmod(i, QUANT_TILES)
+            if r == 0:
                 grouped = work.tile(
-                    [P, GROUP, PASSES, P, PACK], BF16, name="grouped", align_bytes=64
+                    [P, QUANT_TILES, PASSES, P, PACK], BF16, name="grouped", align_bytes=64
                 )
-                grouped_tiles[group] = grouped
-            for g in range(PASSES):
-                nc.vector.tensor_tensor(
-                    out=grouped_tiles[group][:, n, g],
-                    in0=yT_tiles[i][g][:].rearrange("p t r -> p r t"),
-                    in1=ln_w_cols[:, g].unsqueeze(1).to_broadcast([P, P, PACK]),
-                    op=ALU.mult,
-                )
+                grouped_tiles[m] = grouped
+            nc.scalar.copy(
+                out=grouped_tiles[m][:, r].bitcast(F32),
+                in_=hT_tiles[i][:].rearrange("p (g u) r -> p g r u", u=PAIR),
+            )
 
-        def quantise(group):
-            codes = work.tile([P, GROUP * PASSES * P], U32, name="codes", align_bytes=64)
-            scales = work.tile([P, GROUP * PASSES * P], U8, name="scales", align_bytes=64)
+        def quantise(m):
+            codes = work.tile([P, QUANT_TILES * PASSES * P], U32, name="codes", align_bytes=64)
+            scales = work.tile([P, QUANT_TILES * PASSES * P], U8, name="scales", align_bytes=64)
             nc.vector.quantize_mx(
                 out=codes[:].bitcast(FP8X4),
                 scales=scales[:],
-                in_=grouped_tiles[group][:].rearrange("p n g r t -> p (n g r t)"),
+                in_=grouped_tiles[m][:].rearrange("p n g r t -> p (n g r t)"),
             )
-            code_tiles[group] = (codes, scales)
+            code_tiles[m] = (codes, scales)
 
         def project(i):
             g, n = divmod(i, GROUP)
-            codes, scales = code_tiles[g]
+            m, r = divmod(i, QUANT_TILES)
+            codes, scales = code_tiles[m]
             if n == 0:
                 acc_v = psum_v.tile([P, GROUP, HD], F32, name="acc_v")
                 acc_v_tiles[g] = acc_v
             acc_qk = psum_qk.tile([P, ROTATED], F32, name="acc_qk")
+            acc_qk_tiles[i] = acc_qk
             for out, cols in (
                 (acc_qk[:], slice(0, ROTATED)),
                 (acc_v_tiles[g][:, n, :], slice(ROTATED, W_COLS)),
             ):
                 for c in range(PASSES):
-                    tokens = slice((n * PASSES + c) * P, (n * PASSES + c + 1) * P)
+                    tokens = slice((r * PASSES + c) * P, (r * PASSES + c + 1) * P)
                     nc.tensor.matmul_mx(
                         out=out,
                         lhsT=codes[:, tokens].bitcast(FP8X4),
@@ -250,15 +241,14 @@ def tile_nexamodel_pa_t_kernel(
                         start=(c == 0),
                         stop=(c == PASSES - 1),
                     )
-            return acc_qk
 
-        def rope_products(i, acc_qk):
-            m = i % TABLE_TILES
-            products = work.tile([P, 2, 2, HD], F32, name="products")
+        def rope_products(i):
+            pairs = HD // 2
+            products = work.tile([P, 2, pairs, 4], F32, name="products")
             nc.vector.tensor_tensor(
                 out=products[:],
-                in0=acc_qk[:].rearrange("p (s c d) -> p s c d", s=2, c=2),
-                in1=tables[:, :, m, :].unsqueeze(2).to_broadcast([P, 2, 2, HD]),
+                in0=acc_qk_tiles[i][:].rearrange("p (s i f) -> p s i f", s=2, f=4),
+                in1=cos_sin[:, :, i % TABLE_TILES, :].unsqueeze(3).to_broadcast([P, 2, pairs, 4]),
                 op=ALU.mult,
             )
             product_tiles[i] = products
@@ -268,10 +258,13 @@ def tile_nexamodel_pa_t_kernel(
             if n == 0:
                 rotated = work.tile([P, 2, GROUP, HD], F32, name="rotated")
                 result_tiles[g] = rotated
+            cos_part, sin_part = (
+                product_tiles[i][:, s].rearrange("p i (c e) -> p c i e", c=2) for s in range(2)
+            )
             nc.gpsimd.tensor_tensor(
-                out=result_tiles[g][:, :, n, :],
-                in0=product_tiles[i][:, 0],
-                in1=product_tiles[i][:, 1],
+                out=result_tiles[g][:, :, n, :].rearrange("p c (i e) -> p c i e", e=2),
+                in0=cos_part,
+                in1=sin_part,
                 op=ALU.add,
             )
 
@@ -286,32 +279,39 @@ def tile_nexamodel_pa_t_kernel(
             return 0 <= i < N_TILES
 
         with tc.manual_schedule():
-            prepare_constants()
-            for i in range(GROUP):
+            nc.vector.memset(eps[:], EPS)
+            warm = const.tile([P, 1], F32, name="warm")
+            nc.scalar.activation(out=warm[:], in_=eps[:], func=ACT.Abs_reciprocal_sqrt)
+            start_loads()
+            make_identity(nc, ident[:])
+            for i in range(STATS_LEAD):
                 sum_squares(i)
-            inverse_rms(0)
-            quantise_weights()
-            for step in range(GROUP - STATS_LEAD, N_TILES + 8):
+                if i % QUANT_TILES == QUANT_TILES - 1:
+                    inverse_rms(i // QUANT_TILES)
+            group_weights()
+            for step in range(N_TILES + PROJECT_LAG + 1):
                 ahead = step + STATS_LEAD
+                done = step - PROJECT_LAG
                 if exists(ahead) and ahead % GROUP == 0 and ahead // GROUP + 2 < N_GROUPS:
                     load_group(ahead // GROUP + 2)
-                if exists(step - 6):
-                    acc_qk = project(step - 6)
+                if exists(done):
+                    project(done)
                 if exists(step):
+                    normalise(step)
                     transpose(step)
-                if exists(step - 1):
-                    weigh_and_regroup(step - 1)
-                if exists(step - 2) and (step - 2) % GROUP == GROUP - 1:
-                    quantise((step - 2) // GROUP)
-                if exists(step - 6):
-                    rope_products(step - 6, acc_qk)
-                if exists(step - 7):
-                    rope_sum(step - 7)
-                    if (step - 7) % GROUP == GROUP - 1:
-                        store_group((step - 7) // GROUP)
-                if exists(step + 1):
-                    scale_rows(step + 1)
+                if step == 1:
+                    quantise_weights()
                 if exists(ahead):
                     sum_squares(ahead)
-                    if ahead % GROUP == GROUP - 1:
-                        inverse_rms(ahead // GROUP)
+                if exists(step):
+                    regroup(step)
+                if exists(ahead) and ahead % QUANT_TILES == QUANT_TILES - 1:
+                    inverse_rms(ahead // QUANT_TILES)
+                if exists(done):
+                    rope_products(done)
+                if exists(step - 1) and step % QUANT_TILES == 0:
+                    quantise(step // QUANT_TILES - 1)
+                if exists(done):
+                    rope_sum(done)
+                    if done % GROUP == GROUP - 1:
+                        store_group(done // GROUP)

@@ -50,13 +50,16 @@ def tile_nexamodel_pa_t_kernel(
         stat_pool = ctx.enter_context(tc.tile_pool(name="stat", bufs=4))
         scratch_pool = ctx.enter_context(tc.tile_pool(name="scratch", bufs=2))
         work = ctx.enter_context(tc.tile_pool(name="work", bufs=3))
-        psum_t = ctx.enter_context(tc.psum_pool(name="psum_t", bufs=3))
+        psum_const = ctx.enter_context(tc.psum_pool(name="psum_const", bufs=1))
+        psum_t = ctx.enter_context(tc.psum_pool(name="psum_t", bufs=2))
         psum_qk = ctx.enter_context(tc.psum_pool(name="psum_qk", bufs=3))
         psum_v = ctx.enter_context(tc.psum_pool(name="psum_v", bufs=2))
 
         eps = const.tile([P, 1], F32, name="eps")
         ident = const.tile([P, P], F32, name="ident")
-        ln_w_rows = const.tile([P, C], BF16, name="ln_w_rows")
+        ones = const.tile([P, P], BF16, name="ones")
+        ln_w_row = const.tile([P, C], BF16, name="ln_w_row")
+        ln_w_all = psum_const.tile([P, C], BF16, name="ln_w_all")
         cos_sin = const.tile([P, 2, TABLE_TILES, HD // 2], BF16, name="cos_sin")
         w_raw = const.tile([P, 3, PASSES, PACK, HD], BF16, name="w_raw")
         w_grouped = const.tile([P, PASSES, W_COLS, PACK], BF16, name="w_grouped", align_bytes=64)
@@ -88,7 +91,7 @@ def tile_nexamodel_pa_t_kernel(
             load_tile(1)
             load_weight(0, wq)
             load_weight(1, wk)
-            nc.sync.dma_start(out=ln_w_rows[:], in_=ln_w.partition_broadcast(P))
+            nc.sync.dma_start(out=ln_w_row[0:1, :], in_=ln_w.unsqueeze(0))
             load_tile(2)
             load_weight(2, wv)
             load_tile(3)
@@ -99,6 +102,14 @@ def tile_nexamodel_pa_t_kernel(
                 )
             load_group(1)
             load_group(2)
+
+        def spread_ln_w():
+            half = C // 2
+            for c in range(2):
+                cols = slice(c * half, (c + 1) * half)
+                nc.tensor.matmul(
+                    ln_w_all[:, cols], lhsT=ones[:], rhs=ln_w_row[:, cols], start=True, stop=True
+                )
 
         def group_weights():
             rotated = w_grouped[:, :, 0:ROTATED, :].rearrange(
@@ -176,7 +187,7 @@ def tile_nexamodel_pa_t_kernel(
                 out=h[:],
                 in0=x_tiles[g][:, n, :],
                 scalar=inv_rms_tiles[m][:, r : r + 1],
-                in1=ln_w_rows[:],
+                in1=ln_w_all[:],
                 op0=ALU.mult,
                 op1=ALU.mult,
             )
@@ -282,7 +293,10 @@ def tile_nexamodel_pa_t_kernel(
             nc.vector.memset(eps[:], EPS)
             warm = const.tile([P, 1], F32, name="warm")
             nc.scalar.activation(out=warm[:], in_=eps[:], func=ACT.Abs_reciprocal_sqrt)
+            nc.vector.memset(ln_w_row[:], 0.0)
+            nc.vector.memset(ones[:], 1.0)
             start_loads()
+            spread_ln_w()
             make_identity(nc, ident[:])
             for i in range(STATS_LEAD):
                 sum_squares(i)

@@ -27,9 +27,11 @@ N_GROUPS = N_TILES // GROUP
 TABLE_TILES = SEQ // P
 QUANT_TILES = 2
 STATS_LEAD = 3
-PROJECT_LAG = 3
+PROJECT_LAG = 4
 ROTATED = 4 * HD
 W_COLS = ROTATED + HD
+PLAIN = 2 * HD
+GPSIMD_ROPE_TILE = 1
 
 FLOPS = 2 * TOKENS * C * 3 * HD
 
@@ -60,6 +62,8 @@ def tile_nexamodel_pa_t_kernel(
         ones = const.tile([P, P], BF16, name="ones")
         ln_w_row = const.tile([P, C], BF16, name="ln_w_row")
         ln_w_all = psum_const.tile([P, C], BF16, name="ln_w_all")
+        sin_signs = const.tile([P, 2], F32, name="sin_signs")
+        signed_sin = const.tile([P, TABLE_TILES, HD // 2, 2], BF16, name="signed_sin")
         cos_sin = const.tile([P, 2, TABLE_TILES, HD // 2], BF16, name="cos_sin")
         w_raw = const.tile([P, 3, PASSES, PACK, HD], BF16, name="w_raw")
         w_grouped = const.tile([P, PASSES, W_COLS, PACK], BF16, name="w_grouped", align_bytes=64)
@@ -136,6 +140,20 @@ def tile_nexamodel_pa_t_kernel(
                 in_=w_raw[:, 2].rearrange("p g t n -> p g n t"),
             )
 
+        def sign_sin():
+            nc.gpsimd.memset(sin_signs[:, 0:1], -1.0)
+            nc.gpsimd.memset(sin_signs[:, 1:2], 1.0)
+            values = TABLE_TILES * HD // 2
+            nc.gpsimd.tensor_tensor(
+                out=signed_sin[:].rearrange("p m i e -> p (m i) e"),
+                in0=cos_sin[:, 1]
+                .rearrange("p m i -> p (m i)")
+                .unsqueeze(2)
+                .to_broadcast([P, values, 2]),
+                in1=sin_signs[:].unsqueeze(1).to_broadcast([P, values, 2]),
+                op=ALU.mult,
+            )
+
         def quantise_weights():
             for g in range(PASSES):
                 for cols in (slice(0, ROTATED), slice(ROTATED, W_COLS)):
@@ -151,6 +169,7 @@ def tile_nexamodel_pa_t_kernel(
         code_tiles = {}
         acc_qk_tiles = {}
         acc_v_tiles = {}
+        qk_tiles = {}
         product_tiles = {}
         result_tiles = {}
 
@@ -237,8 +256,9 @@ def tile_nexamodel_pa_t_kernel(
                 acc_v_tiles[g] = acc_v
             acc_qk = psum_qk.tile([P, ROTATED], F32, name="acc_qk")
             acc_qk_tiles[i] = acc_qk
+            rotated_cols = PLAIN if n == GPSIMD_ROPE_TILE else ROTATED
             for out, cols in (
-                (acc_qk[:], slice(0, ROTATED)),
+                (acc_qk[:, 0:rotated_cols], slice(0, rotated_cols)),
                 (acc_v_tiles[g][:, n, :], slice(ROTATED, W_COLS)),
             ):
                 for c in range(PASSES):
@@ -260,6 +280,29 @@ def tile_nexamodel_pa_t_kernel(
                 out=products[:],
                 in0=acc_qk_tiles[i][:].rearrange("p (s i f) -> p s i f", s=2, f=4),
                 in1=cos_sin[:, :, i % TABLE_TILES, :].unsqueeze(3).to_broadcast([P, 2, pairs, 4]),
+                op=ALU.mult,
+            )
+            product_tiles[i] = products
+
+        def copy_qk(i):
+            qk = work.tile([P, PLAIN], F32, name="qk")
+            nc.scalar.copy(out=qk[:], in_=acc_qk_tiles[i][:, 0:PLAIN])
+            qk_tiles[i] = qk
+
+        def rope_products_on_gpsimd(i):
+            pairs = HD // 2
+            m = i % TABLE_TILES
+            products = work.tile([P, 2, pairs, 4], F32, name="products")
+            nc.gpsimd.tensor_tensor(
+                out=products[:, 0],
+                in0=qk_tiles[i][:].rearrange("p (i f) -> p i f", f=4),
+                in1=cos_sin[:, 0, m, :].unsqueeze(2).to_broadcast([P, pairs, 4]),
+                op=ALU.mult,
+            )
+            nc.gpsimd.tensor_tensor(
+                out=products[:, 1].rearrange("p i (c e) -> p i c e", c=2),
+                in0=qk_tiles[i][:].rearrange("p (i c e) -> p i c e", c=2, e=2)[:, :, :, ::-1],
+                in1=signed_sin[:, m].unsqueeze(2).to_broadcast([P, pairs, 2, 2]),
                 op=ALU.mult,
             )
             product_tiles[i] = products
@@ -303,6 +346,7 @@ def tile_nexamodel_pa_t_kernel(
                 if i % QUANT_TILES == QUANT_TILES - 1:
                     inverse_rms(i // QUANT_TILES)
             group_weights()
+            sign_sin()
             for step in range(N_TILES + PROJECT_LAG + 1):
                 ahead = step + STATS_LEAD
                 done = step - PROJECT_LAG
@@ -317,14 +361,19 @@ def tile_nexamodel_pa_t_kernel(
                     quantise_weights()
                 if exists(ahead):
                     sum_squares(ahead)
+                gpsimd_rope = exists(done) and done % GROUP == GPSIMD_ROPE_TILE
+                if gpsimd_rope:
+                    copy_qk(done)
                 if exists(step):
                     regroup(step)
                 if exists(ahead) and ahead % QUANT_TILES == QUANT_TILES - 1:
                     inverse_rms(ahead // QUANT_TILES)
-                if exists(done):
+                if exists(done) and not gpsimd_rope:
                     rope_products(done)
-                if exists(step - 1) and step % QUANT_TILES == 0:
+                if exists(step - 2) and step % QUANT_TILES == 1:
                     quantise(step // QUANT_TILES - 1)
+                if gpsimd_rope:
+                    rope_products_on_gpsimd(done)
                 if exists(done):
                     rope_sum(done)
                     if done % GROUP == GROUP - 1:

@@ -20,6 +20,7 @@ SEQ = 2048
 C = 1024
 PASSES = C // K_PASS
 HD = 128
+BANK = 512
 EPS = 1e-6
 GROUP = 4
 N_TILES = TOKENS // P
@@ -28,9 +29,8 @@ TABLE_TILES = SEQ // P
 QUANT_TILES = 2
 STATS_LEAD = 3
 PROJECT_LAG = 4
-ROTATED = 4 * HD
+ROTATED = 2 * HD
 W_COLS = ROTATED + HD
-PLAIN = 2 * HD
 GPSIMD_ROPE_TILE = 1
 
 FLOPS = 2 * TOKENS * C * 3 * HD
@@ -65,7 +65,7 @@ def tile_nexamodel_pa_t_kernel(
         sin_signs = const.tile([P, 2], F32, name="sin_signs")
         signed_sin = const.tile([P, TABLE_TILES, HD // 2, 2], BF16, name="signed_sin")
         cos_sin = const.tile([P, 2, TABLE_TILES, HD // 2], BF16, name="cos_sin")
-        w_raw = const.tile([P, 3, PASSES, PACK, HD], BF16, name="w_raw")
+        w_raw = const.tile([P, 3, PASSES * PACK, HD], BF16, name="w_raw")
         w_grouped = const.tile([P, PASSES, W_COLS, PACK], BF16, name="w_grouped", align_bytes=64)
         w_codes = const.tile([P, PASSES, W_COLS], U32, name="w_codes", align_bytes=64)
         w_scales = const.tile([P, PASSES, W_COLS], U8, name="w_scales", align_bytes=64)
@@ -88,7 +88,8 @@ def tile_nexamodel_pa_t_kernel(
 
             def load_weight(j, w):
                 nc.sync.dma_start(
-                    out=w_raw[:, j], in_=w.rearrange("(g p t) n -> p g t n", t=PACK, p=P)
+                    out=w_raw[:, j].rearrange("p (g u e) n -> p (g u) (e n)", u=PAIR, e=PAIR),
+                    in_=w.rearrange("(g p e) n -> p g (e n)", p=P, e=PAIR),
                 )
 
             load_tile(0)
@@ -116,29 +117,11 @@ def tile_nexamodel_pa_t_kernel(
                 )
 
         def group_weights():
-            rotated = w_grouped[:, :, 0:ROTATED, :].rearrange(
-                "p g (s i c e) t -> p g s i c e t", s=2, c=2, e=2
-            )
-            for j in (0, 1):
-                for g in range(PASSES):
-                    nc.vector.tensor_copy(
-                        out=rotated[:, g, 0, :, j],
-                        in_=w_raw[:, j, g].rearrange("p t (i e) -> p i e t", e=2),
-                    )
-                plain = w_raw[:, j].rearrange("p g t (i e) -> p g i e t", e=2)
-                for e, sign in ((0, -1.0), (1, 1.0)):
-                    nc.gpsimd.tensor_scalar(
-                        out=rotated[:, :, 1, :, j, e, :],
-                        in0=plain[:, :, :, 1 - e, :],
-                        scalar1=sign,
-                        scalar2=0.0,
-                        op0=ALU.mult,
-                        op1=ALU.add,
-                    )
-            nc.vector.tensor_copy(
-                out=w_grouped[:, :, ROTATED:W_COLS, :],
-                in_=w_raw[:, 2].rearrange("p g t n -> p g n t"),
-            )
+            for j in range(3):
+                nc.vector.tensor_copy(
+                    out=w_grouped[:, :, j * HD : (j + 1) * HD, :],
+                    in_=w_raw[:, j].rearrange("p (g t) n -> p g n t", t=PACK),
+                )
 
         def sign_sin():
             nc.gpsimd.memset(sin_signs[:, 0:1], -1.0)
@@ -155,13 +138,15 @@ def tile_nexamodel_pa_t_kernel(
             )
 
         def quantise_weights():
-            for g in range(PASSES):
-                for cols in (slice(0, ROTATED), slice(ROTATED, W_COLS)):
-                    nc.vector.quantize_mx(
-                        out=w_codes[:, g, cols].bitcast(FP8X4),
-                        scales=w_scales[:, g, cols],
-                        in_=w_grouped[:, g, cols, :].rearrange("p c t -> p (c t)"),
-                    )
+            codes = w_codes[:].rearrange("p g c -> p (g c)")
+            scales = w_scales[:].rearrange("p g c -> p (g c)")
+            grouped = w_grouped[:].rearrange("p g c t -> p (g c t)")
+            for cols in (slice(0, 4 * HD), slice(4 * HD, 6 * HD)):
+                nc.vector.quantize_mx(
+                    out=codes[:, cols].bitcast(FP8X4),
+                    scales=scales[:, cols],
+                    in_=grouped[:, cols.start * PACK : cols.stop * PACK],
+                )
 
         h_tiles = {}
         hT_tiles = {}
@@ -215,14 +200,10 @@ def tile_nexamodel_pa_t_kernel(
         def transpose(i):
             words = h_tiles[i][:].bitcast(F32)
             hT = psum_t.tile([P, PASSES * PAIR, P], F32, name="hT")
-            pass_words = K_PASS // PAIR
-            for g in range(PASSES):
-                for u in range(PAIR):
-                    nc.tensor.transpose(
-                        hT[:, g * PAIR + u, :],
-                        words[:, g * pass_words + u : (g + 1) * pass_words : PAIR],
-                        ident[:],
-                    )
+            for block in range(PASSES * PAIR):
+                nc.tensor.transpose(
+                    hT[:, block, :], words[:, block * P : (block + 1) * P], ident[:]
+                )
             hT_tiles[i] = hT
 
         def regroup(i):
@@ -254,11 +235,11 @@ def tile_nexamodel_pa_t_kernel(
             if n == 0:
                 acc_v = psum_v.tile([P, GROUP, HD], F32, name="acc_v")
                 acc_v_tiles[g] = acc_v
-            acc_qk = psum_qk.tile([P, ROTATED], F32, name="acc_qk")
+            bank = psum_qk.tile([P, BANK], F32, name="acc_qk")
+            acc_qk = bank[:, 0:ROTATED]
             acc_qk_tiles[i] = acc_qk
-            rotated_cols = PLAIN if n == GPSIMD_ROPE_TILE else ROTATED
             for out, cols in (
-                (acc_qk[:, 0:rotated_cols], slice(0, rotated_cols)),
+                (acc_qk, slice(0, ROTATED)),
                 (acc_v_tiles[g][:, n, :], slice(ROTATED, W_COLS)),
             ):
                 for c in range(PASSES):
@@ -273,36 +254,29 @@ def tile_nexamodel_pa_t_kernel(
                         stop=(c == PASSES - 1),
                     )
 
-        def rope_products(i):
-            pairs = HD // 2
-            products = work.tile([P, 2, pairs, 4], F32, name="products")
-            nc.vector.tensor_tensor(
-                out=products[:],
-                in0=acc_qk_tiles[i][:].rearrange("p (s i f) -> p s i f", s=2, f=4),
-                in1=cos_sin[:, :, i % TABLE_TILES, :].unsqueeze(3).to_broadcast([P, 2, pairs, 4]),
-                op=ALU.mult,
-            )
-            product_tiles[i] = products
-
         def copy_qk(i):
-            qk = work.tile([P, PLAIN], F32, name="qk")
-            nc.scalar.copy(out=qk[:], in_=acc_qk_tiles[i][:, 0:PLAIN])
+            qk = work.tile([P, ROTATED], F32, name="qk")
+            nc.scalar.copy(out=qk[:], in_=acc_qk_tiles[i])
             qk_tiles[i] = qk
 
-        def rope_products_on_gpsimd(i):
+        def rope_products(i, engine, source):
             pairs = HD // 2
             m = i % TABLE_TILES
-            products = work.tile([P, 2, pairs, 4], F32, name="products")
-            nc.gpsimd.tensor_tensor(
+            products = work.tile([P, 2, 2, pairs, 2], F32, name="products")
+            a = source.rearrange("p (c i e) -> p c i e", c=2, e=2)
+            engine.tensor_tensor(
                 out=products[:, 0],
-                in0=qk_tiles[i][:].rearrange("p (i f) -> p i f", f=4),
-                in1=cos_sin[:, 0, m, :].unsqueeze(2).to_broadcast([P, pairs, 4]),
+                in0=a,
+                in1=cos_sin[:, 0, m, :]
+                .unsqueeze(1)
+                .unsqueeze(3)
+                .to_broadcast([P, 2, pairs, 2]),
                 op=ALU.mult,
             )
-            nc.gpsimd.tensor_tensor(
-                out=products[:, 1].rearrange("p i (c e) -> p i c e", c=2),
-                in0=qk_tiles[i][:].rearrange("p (i c e) -> p i c e", c=2, e=2)[:, :, :, ::-1],
-                in1=signed_sin[:, m].unsqueeze(2).to_broadcast([P, pairs, 2, 2]),
+            engine.tensor_tensor(
+                out=products[:, 1],
+                in0=a[:, :, :, ::-1],
+                in1=signed_sin[:, m].unsqueeze(1).to_broadcast([P, 2, pairs, 2]),
                 op=ALU.mult,
             )
             product_tiles[i] = products
@@ -312,13 +286,10 @@ def tile_nexamodel_pa_t_kernel(
             if n == 0:
                 rotated = work.tile([P, 2, GROUP, HD], F32, name="rotated")
                 result_tiles[g] = rotated
-            cos_part, sin_part = (
-                product_tiles[i][:, s].rearrange("p i (c e) -> p c i e", c=2) for s in range(2)
-            )
             nc.gpsimd.tensor_tensor(
-                out=result_tiles[g][:, :, n, :].rearrange("p c (i e) -> p c i e", e=2),
-                in0=cos_part,
-                in1=sin_part,
+                out=result_tiles[g][:, :, n, :],
+                in0=product_tiles[i][:, 0].rearrange("p c i e -> p c (i e)"),
+                in1=product_tiles[i][:, 1].rearrange("p c i e -> p c (i e)"),
                 op=ALU.add,
             )
 
@@ -369,11 +340,11 @@ def tile_nexamodel_pa_t_kernel(
                 if exists(ahead) and ahead % QUANT_TILES == QUANT_TILES - 1:
                     inverse_rms(ahead // QUANT_TILES)
                 if exists(done) and not gpsimd_rope:
-                    rope_products(done)
+                    rope_products(done, nc.vector, acc_qk_tiles[done])
                 if exists(step - 2) and step % QUANT_TILES == 1:
                     quantise(step // QUANT_TILES - 1)
                 if gpsimd_rope:
-                    rope_products_on_gpsimd(done)
+                    rope_products(done, nc.gpsimd, qk_tiles[done][:])
                 if exists(done):
                     rope_sum(done)
                     if done % GROUP == GROUP - 1:

@@ -27,7 +27,7 @@ N_TILES = TOKENS // P
 N_GROUPS = N_TILES // GROUP
 TABLE_TILES = SEQ // P
 QUANT_TILES = 2
-STATS_LEAD = 3
+STATS_LEAD = 5
 PROJECT_LAG = 4
 ROTATED = 2 * HD
 W_COLS = ROTATED + HD
@@ -53,8 +53,8 @@ def tile_nexamodel_pa_t_kernel(
         scratch_pool = ctx.enter_context(tc.tile_pool(name="scratch", bufs=2))
         work = ctx.enter_context(tc.tile_pool(name="work", bufs=3))
         psum_const = ctx.enter_context(tc.psum_pool(name="psum_const", bufs=1))
-        psum_t = ctx.enter_context(tc.psum_pool(name="psum_t", bufs=2))
-        psum_qk = ctx.enter_context(tc.psum_pool(name="psum_qk", bufs=3))
+        psum_t = ctx.enter_context(tc.psum_pool(name="psum_t", bufs=3))
+        psum_qk = ctx.enter_context(tc.psum_pool(name="psum_qk", bufs=2))
         psum_v = ctx.enter_context(tc.psum_pool(name="psum_v", bufs=2))
 
         eps = const.tile([P, 1], F32, name="eps")
@@ -105,8 +105,8 @@ def tile_nexamodel_pa_t_kernel(
                     out=cos_sin[:, j].rearrange("p (m n) i -> p m (n i)", n=GROUP),
                     in_=f.rearrange("(m p n) i -> p m (n i)", p=P, n=GROUP),
                 )
-            load_group(1)
-            load_group(2)
+            for g in range(1, 3 + (STATS_LEAD - 1) // GROUP):
+                load_group(g)
 
         def spread_ln_w():
             half = C // 2
@@ -335,8 +335,8 @@ def tile_nexamodel_pa_t_kernel(
                 gpsimd_rope = exists(done) and done % GROUP == GPSIMD_ROPE_TILE
                 if gpsimd_rope:
                     copy_qk(done)
-                if exists(step):
-                    regroup(step)
+                if exists(step - 1):
+                    regroup(step - 1)
                 if exists(ahead) and ahead % QUANT_TILES == QUANT_TILES - 1:
                     inverse_rms(ahead // QUANT_TILES)
                 if exists(done) and not gpsimd_rope:

@@ -20,7 +20,6 @@ SEQ = 2048
 C = 1024
 PASSES = C // K_PASS
 HD = 128
-BANK = 512
 EPS = 1e-6
 GROUP = 4
 N_TILES = TOKENS // P
@@ -31,7 +30,8 @@ STATS_LEAD = 5
 PROJECT_LAG = 4
 ROTATED = 2 * HD
 W_COLS = ROTATED + HD
-GPSIMD_ROPE_TILE = 1
+ROPE_LAG = 6
+GPSIMD_ROPE_PAIR = 1
 
 FLOPS = 2 * TOKENS * C * 3 * HD
 
@@ -94,18 +94,18 @@ def tile_nexamodel_pa_t_kernel(
 
             load_tile(0)
             load_tile(1)
-            load_weight(0, wq)
-            load_weight(1, wk)
             nc.sync.dma_start(out=ln_w_row[0:1, :], in_=ln_w.unsqueeze(0))
             load_tile(2)
-            load_weight(2, wv)
             load_tile(3)
+            load_group(1)
+            for j, w in enumerate((wq, wk, wv)):
+                load_weight(j, w)
             for j, f in enumerate((freqs_cos, freqs_sin)):
                 nc.sync.dma_start(
                     out=cos_sin[:, j].rearrange("p (m n) i -> p m (n i)", n=GROUP),
                     in_=f.rearrange("(m p n) i -> p m (n i)", p=P, n=GROUP),
                 )
-            for g in range(1, 3 + (STATS_LEAD - 1) // GROUP):
+            for g in range(2, 3 + (STATS_LEAD - 1) // GROUP):
                 load_group(g)
 
         def spread_ln_w():
@@ -117,11 +117,21 @@ def tile_nexamodel_pa_t_kernel(
                 )
 
         def group_weights():
-            for j in range(3):
-                nc.vector.tensor_copy(
-                    out=w_grouped[:, :, j * HD : (j + 1) * HD, :],
-                    in_=w_raw[:, j].rearrange("p (g t) n -> p g n t", t=PACK),
-                )
+            rotated = w_grouped[:, :, 0:ROTATED, :].rearrange(
+                "p g (i c e) t -> p g i c e t", c=2, e=2
+            )
+            for j in range(2):
+                for g in range(PASSES):
+                    nc.vector.tensor_copy(
+                        out=rotated[:, g, :, j],
+                        in_=w_raw[:, j, g * PACK : (g + 1) * PACK].rearrange(
+                            "p t (i e) -> p i e t", e=2
+                        ),
+                    )
+            nc.vector.tensor_copy(
+                out=w_grouped[:, :, ROTATED:W_COLS, :],
+                in_=w_raw[:, 2].rearrange("p (g t) n -> p g n t", t=PACK),
+            )
 
         def sign_sin():
             nc.gpsimd.memset(sin_signs[:, 0:1], -1.0)
@@ -169,6 +179,20 @@ def tile_nexamodel_pa_t_kernel(
                 out=squares[:],
                 in_=x_tiles[g][:, n, :],
                 func=ACT.Square,
+                accum_out=sumsq_tiles[m][:, r : r + 1],
+            )
+
+        def sum_squares_on_vector(i):
+            g, n = divmod(i, GROUP)
+            m, r = divmod(i, QUANT_TILES)
+            squares = scratch_pool.tile([P, C], BF16, name="squares_v")
+            nc.vector.scalar_tensor_tensor(
+                out=squares[:],
+                in0=x_tiles[g][:, n, :],
+                scalar=1.0,
+                in1=x_tiles[g][:, n, :],
+                op0=ALU.mult,
+                op1=ALU.mult,
                 accum_out=sumsq_tiles[m][:, r : r + 1],
             )
 
@@ -235,11 +259,11 @@ def tile_nexamodel_pa_t_kernel(
             if n == 0:
                 acc_v = psum_v.tile([P, GROUP, HD], F32, name="acc_v")
                 acc_v_tiles[g] = acc_v
-            bank = psum_qk.tile([P, BANK], F32, name="acc_qk")
-            acc_qk = bank[:, 0:ROTATED]
-            acc_qk_tiles[i] = acc_qk
+            if r == 0:
+                acc_qk = psum_qk.tile([P, QUANT_TILES, ROTATED], F32, name="acc_qk")
+                acc_qk_tiles[m] = acc_qk
             for out, cols in (
-                (acc_qk, slice(0, ROTATED)),
+                (acc_qk_tiles[m][:, r, :], slice(0, ROTATED)),
                 (acc_v_tiles[g][:, n, :], slice(ROTATED, W_COLS)),
             ):
                 for c in range(PASSES):
@@ -254,42 +278,60 @@ def tile_nexamodel_pa_t_kernel(
                         stop=(c == PASSES - 1),
                     )
 
-        def copy_qk(i):
-            qk = work.tile([P, ROTATED], F32, name="qk")
-            nc.scalar.copy(out=qk[:], in_=acc_qk_tiles[i])
-            qk_tiles[i] = qk
+        def copy_qk(m):
+            qk = work.tile([P, QUANT_TILES, ROTATED], F32, name="qk")
+            nc.scalar.copy(out=qk[:], in_=acc_qk_tiles[m][:])
+            qk_tiles[m] = qk
 
-        def rope_products(i, engine, source):
-            pairs = HD // 2
-            m = i % TABLE_TILES
-            products = work.tile([P, 2, 2, pairs, 2], F32, name="products")
-            a = source.rearrange("p (c i e) -> p c i e", c=2, e=2)
+        def rope_products(engine, out, a, first, count):
+            tables = slice(first % TABLE_TILES, first % TABLE_TILES + count)
+            values = count * HD // 2
             engine.tensor_tensor(
-                out=products[:, 0],
-                in0=a,
-                in1=cos_sin[:, 0, m, :]
-                .unsqueeze(1)
-                .unsqueeze(3)
-                .to_broadcast([P, 2, pairs, 2]),
+                out=out[:, 0].rearrange("p n (i f) -> p (n i) f", f=4),
+                in0=a.rearrange("p n (i f) -> p (n i) f", f=4),
+                in1=cos_sin[:, 0, tables, :]
+                .rearrange("p n i -> p (n i)")
+                .unsqueeze(2)
+                .to_broadcast([P, values, 4]),
                 op=ALU.mult,
             )
             engine.tensor_tensor(
-                out=products[:, 1],
-                in0=a[:, :, :, ::-1],
-                in1=signed_sin[:, m].unsqueeze(1).to_broadcast([P, 2, pairs, 2]),
+                out=out[:, 1].rearrange("p n (i c e) -> p (n i) c e", c=2, e=2),
+                in0=a.rearrange("p n (i c e) -> p (n i) c e", c=2, e=2)[:, :, :, ::-1],
+                in1=signed_sin[:, tables]
+                .rearrange("p n i e -> p (n i) e")
+                .unsqueeze(2)
+                .to_broadcast([P, values, 2, 2]),
                 op=ALU.mult,
             )
-            product_tiles[i] = products
+
+        def rope_of_pair(m):
+            products = work.tile([P, 2, QUANT_TILES, ROTATED], F32, name="products")
+            product_tiles[m] = products
+            first = m * QUANT_TILES
+            if on_gpsimd(m):
+                for r in range(QUANT_TILES):
+                    n = slice(r, r + 1)
+                    rope_products(
+                        nc.gpsimd, products[:, :, n, :], qk_tiles[m][:, n, :], first + r, 1
+                    )
+            else:
+                rope_products(nc.vector, products[:], acc_qk_tiles[m][:], first, QUANT_TILES)
 
         def rope_sum(i):
             g, n = divmod(i, GROUP)
+            m, r = divmod(i, QUANT_TILES)
             if n == 0:
                 rotated = work.tile([P, 2, GROUP, HD], F32, name="rotated")
                 result_tiles[g] = rotated
+            cos_part, sin_part = (
+                product_tiles[m][:, s, r].rearrange("p (i c e) -> p c i e", c=2, e=2)
+                for s in range(2)
+            )
             nc.gpsimd.tensor_tensor(
-                out=result_tiles[g][:, :, n, :],
-                in0=product_tiles[i][:, 0].rearrange("p c i e -> p c (i e)"),
-                in1=product_tiles[i][:, 1].rearrange("p c i e -> p c (i e)"),
+                out=result_tiles[g][:, :, n, :].rearrange("p c (i e) -> p c i e", e=2),
+                in0=cos_part,
+                in1=sin_part,
                 op=ALU.add,
             )
 
@@ -299,6 +341,9 @@ def tile_nexamodel_pa_t_kernel(
             nc.sync.dma_start(out=out_groups[0][g], in_=result_tiles[g][:, 0])
             nc.sync.dma_start(out=out_groups[1][g], in_=result_tiles[g][:, 1])
             nc.sync.dma_start(out=out_groups[2][g], in_=v[:])
+
+        def on_gpsimd(m):
+            return m % 4 == GPSIMD_ROPE_PAIR
 
         def exists(i):
             return 0 <= i < N_TILES
@@ -313,12 +358,13 @@ def tile_nexamodel_pa_t_kernel(
             spread_ln_w()
             make_identity(nc, ident[:])
             for i in range(STATS_LEAD):
-                sum_squares(i)
+                if i == 1:
+                    sum_squares_on_vector(i)
+                else:
+                    sum_squares(i)
                 if i % QUANT_TILES == QUANT_TILES - 1:
                     inverse_rms(i // QUANT_TILES)
-            group_weights()
-            sign_sin()
-            for step in range(N_TILES + PROJECT_LAG + 1):
+            for step in range(N_TILES + ROPE_LAG):
                 ahead = step + STATS_LEAD
                 done = step - PROJECT_LAG
                 if exists(ahead) and ahead % GROUP == 0 and ahead // GROUP + 2 < N_GROUPS:
@@ -328,24 +374,27 @@ def tile_nexamodel_pa_t_kernel(
                 if exists(step):
                     normalise(step)
                     transpose(step)
-                if step == 1:
+                if step == 2:
+                    group_weights()
+                    sign_sin()
+                if step == 3:
                     quantise_weights()
                 if exists(ahead):
                     sum_squares(ahead)
-                gpsimd_rope = exists(done) and done % GROUP == GPSIMD_ROPE_TILE
-                if gpsimd_rope:
-                    copy_qk(done)
+                roped = (step - ROPE_LAG) // QUANT_TILES
+                has_rope = exists(step - ROPE_LAG) and step % QUANT_TILES == 0
+                if has_rope and on_gpsimd(roped):
+                    copy_qk(roped)
                 if exists(step - 1):
                     regroup(step - 1)
                 if exists(ahead) and ahead % QUANT_TILES == QUANT_TILES - 1:
                     inverse_rms(ahead // QUANT_TILES)
-                if exists(done) and not gpsimd_rope:
-                    rope_products(done, nc.vector, acc_qk_tiles[done])
+                if has_rope:
+                    rope_of_pair(roped)
                 if exists(step - 2) and step % QUANT_TILES == 1:
                     quantise(step // QUANT_TILES - 1)
-                if gpsimd_rope:
-                    rope_products(done, nc.gpsimd, qk_tiles[done][:])
-                if exists(done):
-                    rope_sum(done)
-                    if done % GROUP == GROUP - 1:
-                        store_group(done // GROUP)
+                if has_rope:
+                    for i in range(roped * QUANT_TILES, (roped + 1) * QUANT_TILES):
+                        rope_sum(i)
+                    if roped % (GROUP // QUANT_TILES) == GROUP // QUANT_TILES - 1:
+                        store_group(roped * QUANT_TILES // GROUP)

@@ -31,7 +31,7 @@ PROJECT_LAG = 4
 ROTATED = 2 * HD
 W_COLS = ROTATED + HD
 ROPE_LAG = 6
-GPSIMD_ROPE_PAIR = 1
+GPSIMD_ROPE_PAIR = 0
 
 FLOPS = 2 * TOKENS * C * 3 * HD
 
@@ -168,11 +168,15 @@ def tile_nexamodel_pa_t_kernel(
         product_tiles = {}
         result_tiles = {}
 
+        def stat_set(i):
+            count = 2 if i < GROUP else GROUP
+            return i - i % count, i % count, count
+
         def sum_squares(i):
             g, n = divmod(i, GROUP)
-            m, r = divmod(i, QUANT_TILES)
+            m, r, count = stat_set(i)
             if r == 0:
-                sumsq = stat_pool.tile([P, QUANT_TILES], F32, name="sumsq")
+                sumsq = stat_pool.tile([P, count], F32, name="sumsq")
                 sumsq_tiles[m] = sumsq
             squares = scratch_pool.tile([P, C], BF16, name="squares")
             nc.scalar.activation(
@@ -184,7 +188,7 @@ def tile_nexamodel_pa_t_kernel(
 
         def sum_squares_on_vector(i):
             g, n = divmod(i, GROUP)
-            m, r = divmod(i, QUANT_TILES)
+            m, r, count = stat_set(i)
             squares = scratch_pool.tile([P, C], BF16, name="squares_v")
             nc.vector.scalar_tensor_tensor(
                 out=squares[:],
@@ -196,8 +200,11 @@ def tile_nexamodel_pa_t_kernel(
                 accum_out=sumsq_tiles[m][:, r : r + 1],
             )
 
-        def inverse_rms(m):
-            inv_rms = stat_pool.tile([P, QUANT_TILES], F32, name="inv_rms")
+        def inverse_rms(i):
+            m, r, count = stat_set(i)
+            if r != count - 1:
+                return
+            inv_rms = stat_pool.tile([P, count], F32, name="inv_rms")
             nc.scalar.activation(
                 out=inv_rms[:],
                 in_=sumsq_tiles[m][:],
@@ -209,7 +216,7 @@ def tile_nexamodel_pa_t_kernel(
 
         def normalise(i):
             g, n = divmod(i, GROUP)
-            m, r = divmod(i, QUANT_TILES)
+            m, r, count = stat_set(i)
             h = work.tile([P, C], BF16, name="h")
             nc.vector.scalar_tensor_tensor(
                 out=h[:],
@@ -321,26 +328,34 @@ def tile_nexamodel_pa_t_kernel(
         def rope_sum(i):
             g, n = divmod(i, GROUP)
             m, r = divmod(i, QUANT_TILES)
-            if n == 0:
-                rotated = work.tile([P, 2, GROUP, HD], F32, name="rotated")
-                result_tiles[g] = rotated
+            if g == N_GROUPS - 1:
+                if r == 0:
+                    last = work.tile([P, 2, QUANT_TILES, HD], F32, name="last")
+                    result_tiles[m, "pair"] = last
+                result = result_tiles[m, "pair"][:, :, r, :]
+            else:
+                if n == 0:
+                    rotated = work.tile([P, 2, GROUP, HD], F32, name="rotated")
+                    result_tiles[g, "group"] = rotated
+                result = result_tiles[g, "group"][:, :, n, :]
             cos_part, sin_part = (
                 product_tiles[m][:, s, r].rearrange("p (i c e) -> p c i e", c=2, e=2)
                 for s in range(2)
             )
-            nc.gpsimd.tensor_tensor(
-                out=result_tiles[g][:, :, n, :].rearrange("p c (i e) -> p c i e", e=2),
+            engine = nc.vector if i >= N_TILES - QUANT_TILES else nc.gpsimd
+            engine.tensor_tensor(
+                out=result.rearrange("p c (i e) -> p c i e", e=2),
                 in0=cos_part,
                 in1=sin_part,
                 op=ALU.add,
             )
 
-        def store_group(g):
+        def store_tiles(g, tiles, result):
             v = work.tile([P, GROUP, HD], F32, name="v")
-            nc.scalar.copy(out=v[:], in_=acc_v_tiles[g][:])
-            nc.sync.dma_start(out=out_groups[0][g], in_=result_tiles[g][:, 0])
-            nc.sync.dma_start(out=out_groups[1][g], in_=result_tiles[g][:, 1])
-            nc.sync.dma_start(out=out_groups[2][g], in_=v[:])
+            nc.scalar.copy(out=v[:, tiles, :], in_=acc_v_tiles[g][:, tiles, :])
+            nc.sync.dma_start(out=out_groups[2][g][:, tiles, :], in_=v[:, tiles, :])
+            for c in range(2):
+                nc.sync.dma_start(out=out_groups[c][g][:, tiles, :], in_=result[:, c])
 
         def on_gpsimd(m):
             return m % 4 == GPSIMD_ROPE_PAIR
@@ -362,8 +377,7 @@ def tile_nexamodel_pa_t_kernel(
                     sum_squares_on_vector(i)
                 else:
                     sum_squares(i)
-                if i % QUANT_TILES == QUANT_TILES - 1:
-                    inverse_rms(i // QUANT_TILES)
+                inverse_rms(i)
             for step in range(N_TILES + ROPE_LAG):
                 ahead = step + STATS_LEAD
                 done = step - PROJECT_LAG
@@ -387,8 +401,8 @@ def tile_nexamodel_pa_t_kernel(
                     copy_qk(roped)
                 if exists(step - 1):
                     regroup(step - 1)
-                if exists(ahead) and ahead % QUANT_TILES == QUANT_TILES - 1:
-                    inverse_rms(ahead // QUANT_TILES)
+                if exists(ahead):
+                    inverse_rms(ahead)
                 if has_rope:
                     rope_of_pair(roped)
                 if exists(step - 2) and step % QUANT_TILES == 1:
@@ -396,5 +410,8 @@ def tile_nexamodel_pa_t_kernel(
                 if has_rope:
                     for i in range(roped * QUANT_TILES, (roped + 1) * QUANT_TILES):
                         rope_sum(i)
-                    if roped % (GROUP // QUANT_TILES) == GROUP // QUANT_TILES - 1:
-                        store_group(roped * QUANT_TILES // GROUP)
+                    group, r = divmod(roped * QUANT_TILES, GROUP)
+                    if group == N_GROUPS - 1:
+                        store_tiles(group, slice(r, r + QUANT_TILES), result_tiles[roped, "pair"])
+                    elif r + QUANT_TILES == GROUP:
+                        store_tiles(group, slice(0, GROUP), result_tiles[group, "group"])

from contextlib import ExitStack

import concourse.mybir as mybir
from concourse.masks import make_identity

F32 = mybir.dt.float32
BF16 = mybir.dt.bfloat16
U32 = mybir.dt.uint32
U8 = mybir.dt.uint8
FP8X4 = mybir.dt.float8_e4m3fn_x4
ACT = mybir.ActivationFunctionType
ALU = mybir.AluOpType

P = 128
PACK = 4
K_PASS = P * PACK
PAIR = 2
TOKENS = 4 * 2048
SEQ = 2048
C = 1024
PASSES = C // K_PASS
HD = 128
EPS = 1e-6
GROUP = 4
N_TILES = TOKENS // P
N_GROUPS = N_TILES // GROUP
TABLE_TILES = SEQ // P
QUANT_TILES = 2
STATS_LEAD = 5
PROJECT_LAG = 4
ROTATED = 2 * HD
W_COLS = ROTATED + HD
ROPE_LAG = 6
GPSIMD_ROPE_PAIR = 0

FLOPS = 2 * TOKENS * C * 3 * HD


def tile_nexamodel_pa_t_kernel(
    tc, x, freqs_cos, freqs_sin, ln_w, wq, wk, wv, out_0, out_1, out_2
):
    nc = tc.nc
    x_groups = x.flatten_outer_dims().rearrange("(g p n) k -> g p n k", p=P, n=GROUP)
    out_groups = [
        o.flatten_outer_dims().rearrange("(g p n) d -> g p n d", p=P, n=GROUP)
        for o in (out_0, out_1, out_2)
    ]

    with ExitStack() as ctx:
        const = ctx.enter_context(tc.tile_pool(name="const", bufs=1))
        x_pool = ctx.enter_context(tc.tile_pool(name="x", bufs=4))
        stat_pool = ctx.enter_context(tc.tile_pool(name="stat", bufs=4))
        scratch_pool = ctx.enter_context(tc.tile_pool(name="scratch", bufs=2))
        work = ctx.enter_context(tc.tile_pool(name="work", bufs=3))
        psum_const = ctx.enter_context(tc.psum_pool(name="psum_const", bufs=1))
        psum_t = ctx.enter_context(tc.psum_pool(name="psum_t", bufs=3))
        psum_qk = ctx.enter_context(tc.psum_pool(name="psum_qk", bufs=2))
        psum_v = ctx.enter_context(tc.psum_pool(name="psum_v", bufs=2))

        eps = const.tile([P, 1], F32, name="eps")
        ident = const.tile([P, P], F32, name="ident")
        ones = const.tile([P, P], BF16, name="ones")
        ln_w_row = const.tile([P, C], BF16, name="ln_w_row")
        ln_w_all = psum_const.tile([P, C], BF16, name="ln_w_all")
        sin_signs = const.tile([P, 2], F32, name="sin_signs")
        signed_sin = const.tile([P, TABLE_TILES, HD // 2, 2], BF16, name="signed_sin")
        cos_sin = const.tile([P, 2, TABLE_TILES, HD // 2], BF16, name="cos_sin")
        w_raw = const.tile([P, 3, PASSES * PACK, HD], BF16, name="w_raw")
        w_grouped = const.tile([P, PASSES, W_COLS, PACK], BF16, name="w_grouped", align_bytes=64)
        w_codes = const.tile([P, PASSES, W_COLS], U32, name="w_codes", align_bytes=64)
        w_scales = const.tile([P, PASSES, W_COLS], U8, name="w_scales", align_bytes=64)

        x_tiles = {}
        sumsq_tiles = {}
        inv_rms_tiles = {}

        def load_group(g):
            xg = x_pool.tile([P, GROUP, C], BF16, name="xg")
            nc.sync.dma_start(out=xg[:], in_=x_groups[g])
            x_tiles[g] = xg

        def start_loads():
            first_group = x_pool.tile([P, GROUP, C], BF16, name="xg")
            x_tiles[0] = first_group

            def load_tile(n):
                nc.sync.dma_start(out=first_group[:, n, :], in_=x_groups[0][:, n, :])

            def load_weight(j, w):
                nc.sync.dma_start(
                    out=w_raw[:, j].rearrange("p (g u e) n -> p (g u) (e n)", u=PAIR, e=PAIR),
                    in_=w.rearrange("(g p e) n -> p g (e n)", p=P, e=PAIR),
                )

            load_tile(0)
            load_tile(1)
            nc.sync.dma_start(out=ln_w_row[0:1, :], in_=ln_w.unsqueeze(0))
            load_tile(2)
            load_tile(3)
            load_group(1)
            for j, w in enumerate((wq, wk, wv)):
                load_weight(j, w)
            for j, f in enumerate((freqs_cos, freqs_sin)):
                nc.sync.dma_start(
                    out=cos_sin[:, j].rearrange("p (m n) i -> p m (n i)", n=GROUP),
                    in_=f.rearrange("(m p n) i -> p m (n i)", p=P, n=GROUP),
                )
            for g in range(2, 3 + (STATS_LEAD - 1) // GROUP):
                load_group(g)

        def spread_ln_w():
            half = C // 2
            for c in range(2):
                cols = slice(c * half, (c + 1) * half)
                nc.tensor.matmul(
                    ln_w_all[:, cols], lhsT=ones[:], rhs=ln_w_row[:, cols], start=True, stop=True
                )

        def group_weights():
            rotated = w_grouped[:, :, 0:ROTATED, :].rearrange(
                "p g (i c e) t -> p g i c e t", c=2, e=2
            )
            for j in range(2):
                for g in range(PASSES):
                    nc.vector.tensor_copy(
                        out=rotated[:, g, :, j],
                        in_=w_raw[:, j, g * PACK : (g + 1) * PACK].rearrange(
                            "p t (i e) -> p i e t", e=2
                        ),
                    )
            nc.vector.tensor_copy(
                out=w_grouped[:, :, ROTATED:W_COLS, :],
                in_=w_raw[:, 2].rearrange("p (g t) n -> p g n t", t=PACK),
            )

        def sign_sin():
            nc.gpsimd.memset(sin_signs[:, 0:1], -1.0)
            nc.gpsimd.memset(sin_signs[:, 1:2], 1.0)
            values = TABLE_TILES * HD // 2
            nc.gpsimd.tensor_tensor(
                out=signed_sin[:].rearrange("p m i e -> p (m i) e"),
                in0=cos_sin[:, 1]
                .rearrange("p m i -> p (m i)")
                .unsqueeze(2)
                .to_broadcast([P, values, 2]),
                in1=sin_signs[:].unsqueeze(1).to_broadcast([P, values, 2]),
                op=ALU.mult,
            )

        def quantise_weights():
            codes = w_codes[:].rearrange("p g c -> p (g c)")
            scales = w_scales[:].rearrange("p g c -> p (g c)")
            grouped = w_grouped[:].rearrange("p g c t -> p (g c t)")
            for cols in (slice(0, 4 * HD), slice(4 * HD, 6 * HD)):
                nc.vector.quantize_mx(
                    out=codes[:, cols].bitcast(FP8X4),
                    scales=scales[:, cols],
                    in_=grouped[:, cols.start * PACK : cols.stop * PACK],
                )

        h_tiles = {}
        hT_tiles = {}
        grouped_tiles = {}
        code_tiles = {}
        acc_qk_tiles = {}
        acc_v_tiles = {}
        qk_tiles = {}
        product_tiles = {}
        result_tiles = {}

        def stat_set(i):
            count = 2 if i < GROUP else GROUP
            return i - i % count, i % count, count

        def sum_squares(i):
            g, n = divmod(i, GROUP)
            m, r, count = stat_set(i)
            if r == 0:
                sumsq = stat_pool.tile([P, count], F32, name="sumsq")
                sumsq_tiles[m] = sumsq
            squares = scratch_pool.tile([P, C], BF16, name="squares")
            nc.scalar.activation(
                out=squares[:],
                in_=x_tiles[g][:, n, :],
                func=ACT.Square,
                accum_out=sumsq_tiles[m][:, r : r + 1],
            )

        def sum_squares_on_vector(i):
            g, n = divmod(i, GROUP)
            m, r, count = stat_set(i)
            squares = scratch_pool.tile([P, C], BF16, name="squares_v")
            nc.vector.scalar_tensor_tensor(
                out=squares[:],
                in0=x_tiles[g][:, n, :],
                scalar=1.0,
                in1=x_tiles[g][:, n, :],
                op0=ALU.mult,
                op1=ALU.mult,
                accum_out=sumsq_tiles[m][:, r : r + 1],
            )

        def inverse_rms(i):
            m, r, count = stat_set(i)
            if r != count - 1:
                return
            inv_rms = stat_pool.tile([P, count], F32, name="inv_rms")
            nc.scalar.activation(
                out=inv_rms[:],
                in_=sumsq_tiles[m][:],
                func=ACT.Abs_reciprocal_sqrt,
                bias=eps[:],
                scale=1.0 / C,
            )
            inv_rms_tiles[m] = inv_rms

        def normalise(i):
            g, n = divmod(i, GROUP)
            m, r, count = stat_set(i)
            h = work.tile([P, C], BF16, name="h")
            nc.vector.scalar_tensor_tensor(
                out=h[:],
                in0=x_tiles[g][:, n, :],
                scalar=inv_rms_tiles[m][:, r : r + 1],
                in1=ln_w_all[:],
                op0=ALU.mult,
                op1=ALU.mult,
            )
            h_tiles[i] = h

        def transpose(i):
            words = h_tiles[i][:].bitcast(F32)
            hT = psum_t.tile([P, PASSES * PAIR, P], F32, name="hT")
            for block in range(PASSES * PAIR):
                nc.tensor.transpose(
                    hT[:, block, :], words[:, block * P : (block + 1) * P], ident[:]
                )
            hT_tiles[i] = hT

        def regroup(i):
            m, r = divmod(i, QUANT_TILES)
            if r == 0:
                grouped = work.tile(
                    [P, QUANT_TILES, PASSES, P, PACK], BF16, name="grouped", align_bytes=64
                )
                grouped_tiles[m] = grouped
            nc.scalar.copy(
                out=grouped_tiles[m][:, r].bitcast(F32),
                in_=hT_tiles[i][:].rearrange("p (g u) r -> p g r u", u=PAIR),
            )

        def quantise(m):
            codes = work.tile([P, QUANT_TILES * PASSES * P], U32, name="codes", align_bytes=64)
            scales = work.tile([P, QUANT_TILES * PASSES * P], U8, name="scales", align_bytes=64)
            nc.vector.quantize_mx(
                out=codes[:].bitcast(FP8X4),
                scales=scales[:],
                in_=grouped_tiles[m][:].rearrange("p n g r t -> p (n g r t)"),
            )
            code_tiles[m] = (codes, scales)

        def project(i):
            g, n = divmod(i, GROUP)
            m, r = divmod(i, QUANT_TILES)
            codes, scales = code_tiles[m]
            if n == 0:
                acc_v = psum_v.tile([P, GROUP, HD], F32, name="acc_v")
                acc_v_tiles[g] = acc_v
            if r == 0:
                acc_qk = psum_qk.tile([P, QUANT_TILES, ROTATED], F32, name="acc_qk")
                acc_qk_tiles[m] = acc_qk
            for out, cols in (
                (acc_qk_tiles[m][:, r, :], slice(0, ROTATED)),
                (acc_v_tiles[g][:, n, :], slice(ROTATED, W_COLS)),
            ):
                for c in range(PASSES):
                    tokens = slice((r * PASSES + c) * P, (r * PASSES + c + 1) * P)
                    nc.tensor.matmul_mx(
                        out=out,
                        lhsT=codes[:, tokens].bitcast(FP8X4),
                        lhsT_scale=scales[:, tokens],
                        rhs=w_codes[:, c, cols].bitcast(FP8X4),
                        rhs_scale=w_scales[:, c, cols],
                        start=(c == 0),
                        stop=(c == PASSES - 1),
                    )

        def copy_qk(m):
            qk = work.tile([P, QUANT_TILES, ROTATED], F32, name="qk")
            nc.scalar.copy(out=qk[:], in_=acc_qk_tiles[m][:])
            qk_tiles[m] = qk

        def rope_products(engine, out, a, first, count):
            tables = slice(first % TABLE_TILES, first % TABLE_TILES + count)
            values = count * HD // 2
            engine.tensor_tensor(
                out=out[:, 0].rearrange("p n (i f) -> p (n i) f", f=4),
                in0=a.rearrange("p n (i f) -> p (n i) f", f=4),
                in1=cos_sin[:, 0, tables, :]
                .rearrange("p n i -> p (n i)")
                .unsqueeze(2)
                .to_broadcast([P, values, 4]),
                op=ALU.mult,
            )
            engine.tensor_tensor(
                out=out[:, 1].rearrange("p n (i c e) -> p (n i) c e", c=2, e=2),
                in0=a.rearrange("p n (i c e) -> p (n i) c e", c=2, e=2)[:, :, :, ::-1],
                in1=signed_sin[:, tables]
                .rearrange("p n i e -> p (n i) e")
                .unsqueeze(2)
                .to_broadcast([P, values, 2, 2]),
                op=ALU.mult,
            )

        def rope_of_pair(m):
            products = work.tile([P, 2, QUANT_TILES, ROTATED], F32, name="products")
            product_tiles[m] = products
            first = m * QUANT_TILES
            if on_gpsimd(m):
                for r in range(QUANT_TILES):
                    n = slice(r, r + 1)
                    rope_products(
                        nc.gpsimd, products[:, :, n, :], qk_tiles[m][:, n, :], first + r, 1
                    )
            else:
                rope_products(nc.vector, products[:], acc_qk_tiles[m][:], first, QUANT_TILES)

        def rope_sum(i):
            g, n = divmod(i, GROUP)
            m, r = divmod(i, QUANT_TILES)
            if g == N_GROUPS - 1:
                if r == 0:
                    last = work.tile([P, 2, QUANT_TILES, HD], F32, name="last")
                    result_tiles[m, "pair"] = last
                result = result_tiles[m, "pair"][:, :, r, :]
            else:
                if n == 0:
                    rotated = work.tile([P, 2, GROUP, HD], F32, name="rotated")
                    result_tiles[g, "group"] = rotated
                result = result_tiles[g, "group"][:, :, n, :]
            cos_part, sin_part = (
                product_tiles[m][:, s, r].rearrange("p (i c e) -> p c i e", c=2, e=2)
                for s in range(2)
            )
            engine = nc.vector if i >= N_TILES - QUANT_TILES else nc.gpsimd
            engine.tensor_tensor(
                out=result.rearrange("p c (i e) -> p c i e", e=2),
                in0=cos_part,
                in1=sin_part,
                op=ALU.add,
            )

        def store_tiles(g, tiles, result):
            v = work.tile([P, GROUP, HD], F32, name="v")
            nc.scalar.copy(out=v[:, tiles, :], in_=acc_v_tiles[g][:, tiles, :])
            nc.sync.dma_start(out=out_groups[2][g][:, tiles, :], in_=v[:, tiles, :])
            for c in range(2):
                nc.sync.dma_start(out=out_groups[c][g][:, tiles, :], in_=result[:, c])

        def on_gpsimd(m):
            return m % 4 == GPSIMD_ROPE_PAIR

        def exists(i):
            return 0 <= i < N_TILES

        with tc.manual_schedule():
            nc.vector.memset(eps[:], EPS)
            warm = const.tile([P, 1], F32, name="warm")
            nc.scalar.activation(out=warm[:], in_=eps[:], func=ACT.Abs_reciprocal_sqrt)
            nc.vector.memset(ln_w_row[:], 0.0)
            nc.vector.memset(ones[:], 1.0)
            start_loads()
            spread_ln_w()
            make_identity(nc, ident[:])
            for i in range(STATS_LEAD):
                if i == 1:
                    sum_squares_on_vector(i)
                else:
                    sum_squares(i)
                inverse_rms(i)
            for step in range(N_TILES + ROPE_LAG):
                ahead = step + STATS_LEAD
                done = step - PROJECT_LAG
                if exists(ahead) and ahead % GROUP == 0 and ahead // GROUP + 2 < N_GROUPS:
                    load_group(ahead // GROUP + 2)
                if exists(done):
                    project(done)
                if exists(step):
                    normalise(step)
                    transpose(step)
                if step == 2:
                    group_weights()
                    sign_sin()
                if step == 3:
                    quantise_weights()
                if exists(ahead):
                    sum_squares(ahead)
                roped = (step - ROPE_LAG) // QUANT_TILES
                has_rope = exists(step - ROPE_LAG) and step % QUANT_TILES == 0
                if has_rope and on_gpsimd(roped):
                    copy_qk(roped)
                if exists(step - 1):
                    regroup(step - 1)
                if exists(ahead):
                    inverse_rms(ahead)
                if has_rope:
                    rope_of_pair(roped)
                if exists(step - 2) and step % QUANT_TILES == 1:
                    quantise(step // QUANT_TILES - 1)
                if has_rope:
                    for i in range(roped * QUANT_TILES, (roped + 1) * QUANT_TILES):
                        rope_sum(i)
                    group, r = divmod(roped * QUANT_TILES, GROUP)
                    if group == N_GROUPS - 1:
                        store_tiles(group, slice(r, r + QUANT_TILES), result_tiles[roped, "pair"])
                    elif r + QUANT_TILES == GROUP:
                        store_tiles(group, slice(0, GROUP), result_tiles[group, "group"])
